import numpy as np
import ml_dtypes


def mxq(x, axis, fmt="e4m3"):
    dtype, down = {"e4m3": (ml_dtypes.float8_e4m3fn, 7), "e5m2": (ml_dtypes.float8_e5m2, 14)}[fmt]
    v = np.moveaxis(np.asarray(x, np.float32).astype(ml_dtypes.bfloat16).astype(np.float64), axis, -1)
    blocks = v.reshape(v.shape[:-1] + (-1, 32))
    amax = np.abs(blocks).max(-1, keepdims=True)
    byte = np.maximum(np.where(amax > 0, np.frexp(amax)[1] - 1 + 127, 0) - down, 1)
    scale = np.exp2(byte - 127.0)
    codes = (blocks / scale).astype(np.float32).astype(dtype).astype(np.float64)
    return np.moveaxis((codes * scale).reshape(v.shape), -1, axis)


WIDE = False


def mx_kscale(k):
    if not WIDE:
        return np.ones(k)
    levels = np.array([10, -10, 5, -5, 0])
    a = np.random.permutation(np.resize(levels, k // 512 * 4)).reshape(k // 512, 4)
    idx = np.arange(k)
    return np.exp2(a[idx // 512, idx % 128 // 32])


BF16 = ml_dtypes.bfloat16


def bf(x):
    return np.asarray(x, np.float32).astype(BF16)


def f64(x):
    return np.asarray(x).astype(np.float64)


B, S, D, H = 1, 512, 2048, 16
HD = D // H
NEG = -3.4028234663852886e38


def alibi_slopes(num_heads):
    ratio = 2.0 ** (-8.0 / num_heads)
    return ratio ** f64(np.arange(1, num_heads + 1))


def setup_inputs():
    s = mx_kscale(D)
    return {"x": bf(np.random.standard_normal((B, S, D)) * s),
            "Wv": bf(np.random.standard_normal((D, D)) / np.sqrt(D) / s[:, None]),
            "bv": bf(np.random.standard_normal(D) * 0.1),
            "q": bf(np.random.standard_normal((B, H, S, HD))),
            "k": bf(np.random.standard_normal((B, H, S, HD)))}


def reference(x, Wv, bv, q, k):
    v = (mxq(f64(x), 2, "e4m3") @ mxq(f64(Wv), 0, "e4m3")) + f64(bv)
    v = v.reshape(B, S, H, HD).transpose(0, 2, 1, 3)
    scores = f64(q) @ f64(k).transpose(0, 1, 3, 2) / np.sqrt(HD)
    distances = f64(np.arange(1 - S, 1))
    scores = scores + alibi_slopes(H)[None, :, None, None] * distances[None, None, None, :]
    causal = np.tril(np.ones((S, S), dtype=bool))[None, None]
    scores = np.where(causal, scores, NEG)
    e = np.exp(scores - scores.max(-1, keepdims=True))
    ctx = (mxq(e, 3, "e4m3") @ mxq(v, 2, "e4m3")) / e.sum(-1, keepdims=True)
    return ctx.transpose(0, 2, 1, 3).reshape(B, S, D)

@@ -1,0 +1,408 @@
+import concourse.mybir as mybir
+from concourse.masks import make_identity
+
+F32 = mybir.dt.float32
+BF16 = mybir.dt.bfloat16
+I32 = mybir.dt.int32
+U32 = mybir.dt.uint32
+U8 = mybir.dt.uint8
+FP8X4 = mybir.dt.float8_e4m3fn_x4
+ALU = mybir.AluOpType
+ACT = mybir.ActivationFunctionType
+
+P = 128
+S = 512
+D = 2048
+H = 16
+HD = 128
+PACK = 4
+K_PASS = P * PACK
+PASSES = D // K_PASS
+ROW_TILES = S // P
+GROUP = 4
+GROUPS = H // GROUP
+CHUNK = GROUP * HD
+PLANES = D // (2 * P)
+
+SCALE = 1.0 / HD**0.5
+KEY_CENTRE = S // 2
+QUADRANT = 32
+MASK_ROWS = P // 2
+FAINT = 2.0**-78
+MASK_EVEN = -(2.0**48)
+MASK_ODD = -(2.0**126)
+
+FLOPS = 2 * S * D * D + 2 * 2 * H * S * S * HD
+
+
+def raw_slope(head):
+    return 2.0 ** (-(head + 1) / 2.0) / SCALE
+
+
+TURN_QK_AHEAD = 1
+TURN_E_LAG = 2
+LOAD_QK_AHEAD = 3
+W_PASSES = GROUPS * PASSES
+QUANTISE_W_LAG = 1
+PROJECT_LAG = GROUP + QUANTISE_W_LAG
+ATTEND_LAG = PROJECT_LAG + 1
+STEPS = H + ATTEND_LAG
+
+
+def tile_selfattention_pa_kernel(tc, x, Wv, bv, q, k, out):
+    nc = tc.nc
+
+    with tc.tile_pool(name="consts", bufs=1) as consts, tc.tile_pool(
+        name="fixed", bufs=1
+    ) as fixed, tc.tile_pool(name="w_raw", bufs=2) as w_raw_pool, tc.tile_pool(
+        name="w_mx", bufs=2
+    ) as w_mx_pool, tc.tile_pool(name="qk_raw", bufs=LOAD_QK_AHEAD + 1) as qk_raw_pool, tc.tile_pool(
+        name="stage", bufs=3
+    ) as stage, tc.tile_pool(name="e_mx", bufs=ATTEND_LAG - TURN_E_LAG + 2) as e_mx_pool, tc.tile_pool(
+        name="head", bufs=3
+    ) as head_pool, tc.psum_pool(name="score_ps", bufs=1) as score_ps, tc.psum_pool(
+        name="et_ps", bufs=2
+    ) as et_ps, tc.psum_pool(name="turn_ps", bufs=1) as turn_ps, tc.psum_pool(
+        name="v_ps", bufs=1
+    ) as v_ps, tc.psum_pool(name="ctx_ps", bufs=1) as ctx_ps, tc.manual_schedule():
+        q_rows = q.rearrange("b h (c p) d -> p (b h) c d", p=P)
+        k_rows = k.rearrange("b h (c p) d -> p (b h) c d", p=P)
+        w_rows = Wv.rearrange("(l p e) n -> e p l n", l=PLANES, e=2)
+        x_rows = x.rearrange("b (u m e) k -> m (b u) (e k)", u=2, e=2)
+        out_rows = out.rearrange("b (c a) n -> a (b c) n", a=P)
+
+        qk_sb = {}
+        qk_turned = {}
+        w_raw_of = {}
+        w_grouped_of = {}
+        w_mx_of = {}
+        e_mx_of = {}
+        v_grouped_of = {}
+        v_mx_of = {}
+
+        def load_qk(h):
+            q_sb = qk_raw_pool.tile([P, ROW_TILES, HD], BF16, name="q_sb")
+            k_sb = qk_raw_pool.tile([P, ROW_TILES, HD], BF16, name="k_sb")
+            nc.sync.dma_start(out=q_sb[:], in_=q_rows[:, h, :, :])
+            nc.sync.dma_start(out=k_sb[:], in_=k_rows[:, h, :, :])
+            qk_sb[h] = (q_sb, k_sb)
+
+        def load_chunk(group):
+            cols = slice(group * CHUNK, (group + 1) * CHUNK)
+            w_raw = w_raw_pool.tile([P, PLANES, 2, CHUNK], BF16, name="w_raw")
+            for e in range(2):
+                nc.sync.dma_start(out=w_raw[:, :, e, :], in_=w_rows[e, :, :, cols])
+            w_raw_of[group] = w_raw
+
+        for h in range(LOAD_QK_AHEAD):
+            load_qk(h)
+        load_chunk(0)
+        x_sb = fixed.tile([P, ROW_TILES, D], BF16)
+        for u in range(2):
+            nc.sync.dma_start(
+                out=x_sb[:, 2 * u : 2 * u + 2, :].rearrange("m e k -> m (e k)"),
+                in_=x_rows[:, u, :],
+            )
+        bias_rows = consts.tile([P, D], BF16)
+        nc.sync.dma_start(out=bias_rows[:], in_=bv.partition_broadcast(P))
+
+        ident_bf = consts.tile([P, P], BF16)
+        make_identity(nc, ident_bf[:])
+        ident_f32 = consts.tile([P, P], F32)
+        make_identity(nc, ident_f32[:])
+
+        bias_rhs = consts.tile([P, S], BF16)
+        nc.gpsimd.memset(bias_rhs[:MASK_ROWS, :], 0.0)
+        for odd, fill in ((0, MASK_EVEN), (1, MASK_ODD)):
+            nc.gpsimd.affine_select(
+                out=bias_rhs[:MASK_ROWS, :],
+                in_=bias_rhs[:MASK_ROWS, :],
+                compare_op=ALU.not_equal,
+                fill=fill,
+                base=-(S - P) - odd,
+                pattern=[[1, S]],
+                channel_multiplier=-2,
+            )
+        key_numbers = consts.tile([P, S], I32)
+        nc.gpsimd.iota(key_numbers[:], pattern=[[1, S]], base=-KEY_CENTRE, channel_multiplier=0)
+        nc.vector.tensor_scalar(
+            out=bias_rhs[MASK_ROWS:, :],
+            in0=key_numbers[MASK_ROWS:, :],
+            scalar1=1.0 / QUADRANT,
+            scalar2=None,
+            op0=ALU.mult,
+        )
+
+        query_mask = consts.tile([P, P], F32)
+        nc.gpsimd.memset(query_mask[:], 1.0)
+        nc.gpsimd.affine_select(
+            out=query_mask[:],
+            in_=query_mask[:],
+            compare_op=ALU.is_gt,
+            fill=0.0,
+            base=0,
+            pattern=[[-1, P]],
+            channel_multiplier=2,
+        )
+        nc.gpsimd.affine_select(
+            out=query_mask[:],
+            in_=query_mask[:],
+            compare_op=ALU.not_equal,
+            fill=FAINT,
+            base=0,
+            pattern=[[-1, P]],
+            channel_multiplier=2,
+        )
+
+        ones = consts.tile([P, 1], F32)
+        nc.vector.memset(ones[:], 1.0)
+        slope = consts.tile([P, H], F32)
+        for h in range(H):
+            nc.vector.tensor_scalar(
+                out=slope[:, h : h + 1], in0=ones[:], scalar1=raw_slope(h), scalar2=None, op0=ALU.mult
+            )
+        slope_high = consts.tile([P, H], BF16)
+        nc.vector.tensor_copy(out=slope_high[:], in_=slope[:])
+        slope_rest = consts.tile([P, H], F32)
+        nc.vector.tensor_tensor(out=slope_rest[:], in0=slope[:], in1=slope_high[:], op=ALU.subtract)
+
+        bias_lhsT = consts.tile([P, H, P], BF16)
+        nc.vector.tensor_copy(
+            out=bias_lhsT[:MASK_ROWS, :, :],
+            in_=query_mask[:MASK_ROWS, :].unsqueeze(1).to_broadcast([MASK_ROWS, H, P]),
+        )
+        high_rows = slice(MASK_ROWS, MASK_ROWS + QUADRANT)
+        rest_rows = slice(MASK_ROWS + QUADRANT, P)
+        nc.vector.tensor_copy(
+            out=bias_lhsT[high_rows, :, :],
+            in_=slope_high[high_rows, :].unsqueeze(2).to_broadcast([QUADRANT, H, P]),
+        )
+        nc.vector.tensor_copy(
+            out=bias_lhsT[rest_rows, :, :],
+            in_=slope_rest[rest_rows, :].unsqueeze(2).to_broadcast([QUADRANT, H, P]),
+        )
+
+        e_rows = [fixed.tile([P, ROW_TILES, S], BF16, name="e_rows%d" % par) for par in range(2)]
+        for par in range(2):
+            nc.vector.memset(e_rows[par][:].bitcast(I32), 0)
+
+        neg_max = fixed.tile([P, H * ROW_TILES], F32)
+        row_sum = fixed.tile([P, H * ROW_TILES], F32)
+        inv_sum = fixed.tile([P, H * ROW_TILES], F32)
+        x_codes = fixed.tile([P, ROW_TILES, PASSES, P], U32, align_bytes=64)
+        x_scales = fixed.tile([P, ROW_TILES, PASSES, P], U8, align_bytes=64)
+
+        def quantise_x(t):
+            x_words = x_sb[:, t, :].bitcast(F32)
+            for half in range(2):
+                turned = turn_ps.tile([P, 4, P], F32, tag="turned")
+                for w in range(4):
+                    plane = 4 * half + w
+                    nc.tensor.transpose(
+                        turned[:, w, :], x_words[:, plane * P : (plane + 1) * P], ident_f32[:]
+                    )
+                x_grouped = stage.tile([P, 2 * P * PACK], BF16, align_bytes=64)
+                nc.scalar.copy(
+                    out=x_grouped[:].bitcast(F32).rearrange("p (g m u) -> p g m u", g=2, u=2),
+                    in_=turned[:].rearrange("p (g u) m -> p g m u", u=2),
+                )
+                passes = slice(2 * half, 2 * half + 2)
+                nc.vector.quantize_mx(
+                    out=x_codes[:, t, passes, :].rearrange("p g m -> p (g m)").bitcast(FP8X4),
+                    scales=x_scales[:, t, passes, :].rearrange("p g m -> p (g m)"),
+                    in_=x_grouped[:],
+                )
+
+        def regroup_w(n):
+            group, g = divmod(n, PASSES)
+            w_grouped = stage.tile([P, CHUNK, PACK], BF16, align_bytes=64, name="w_grouped")
+            regroup = nc.scalar.copy if n % 2 else nc.vector.tensor_copy
+            regroup(
+                out=w_grouped[:].rearrange("p (c i) t -> p c t i", i=4),
+                in_=w_raw_of[group][:, 2 * g : 2 * g + 2, :, :]
+                .rearrange("p u e n -> p (u e) n")
+                .rearrange("p t (c i) -> p c t i", i=4),
+            )
+            w_grouped_of[n] = w_grouped
+
+        def quantise_w(n):
+            group, g = divmod(n, PASSES)
+            if g == 0:
+                w_codes = w_mx_pool.tile([P, PASSES, CHUNK], U32, align_bytes=64, name="w_codes")
+                w_scales = w_mx_pool.tile([P, PASSES, CHUNK], U8, align_bytes=64, name="w_scales")
+                w_mx_of[group] = (w_codes, w_scales)
+            w_codes, w_scales = w_mx_of[group]
+            nc.vector.quantize_mx(
+                out=w_codes[:, g, :].bitcast(FP8X4),
+                scales=w_scales[:, g, :],
+                in_=w_grouped_of[n][:].rearrange("p n t -> p (n t)"),
+            )
+
+        def turn_qk(h):
+            q_sb, k_sb = qk_sb[h]
+            turned = turn_ps.tile([P, 2 * ROW_TILES, P], BF16, tag="turned")
+            for c in range(ROW_TILES):
+                nc.tensor.transpose(turned[:, c, :], q_sb[:, c, :], ident_bf[:])
+                nc.tensor.transpose(turned[:, ROW_TILES + c, :], k_sb[:, c, :], ident_bf[:])
+            qk_t = head_pool.tile([P, 2 * ROW_TILES, P], BF16, name="qk_t")
+            nc.scalar.copy(out=qk_t[:], in_=turned[:])
+            qk_turned[h] = qk_t
+
+        def scores(h):
+            qk_t = qk_turned[h]
+            score_low = score_ps.tile([P, S], F32, name="score_low")
+            score_mid = score_ps.tile([P, S], F32, name="score_mid")
+            score_high = score_ps.tile([P, S], F32, name="score_high")
+            score_of = [
+                score_low[:, :P],
+                score_low[:, P : 3 * P],
+                score_mid[:, : 3 * P],
+                score_high[:, :],
+            ]
+            for c in range(ROW_TILES):
+                keys = (c + 1) * P
+                nc.tensor.matmul(
+                    score_of[c],
+                    lhsT=qk_t[:, c, :],
+                    rhs=qk_t[:, ROW_TILES : ROW_TILES + c + 1, :].rearrange("d c j -> d (c j)"),
+                    start=True,
+                    stop=False,
+                )
+                nc.tensor.matmul(
+                    score_of[c],
+                    lhsT=bias_lhsT[:, h, :],
+                    rhs=bias_rhs[:, S - keys :],
+                    start=False,
+                    stop=True,
+                )
+            for c in range(ROW_TILES):
+                keys = (c + 1) * P
+                column = h * ROW_TILES + c
+                unused = stage.tile([P, S], BF16, name="unused")
+                nc.vector.tensor_scalar(
+                    out=unused[:, :keys],
+                    in0=score_of[c],
+                    scalar1=-SCALE,
+                    scalar2=None,
+                    op0=ALU.mult,
+                    op1=ALU.min,
+                    accum_out=neg_max[:, column : column + 1],
+                )
+                nc.scalar.activation(
+                    out=e_rows[h % 2][:, c, :keys],
+                    in_=score_of[c],
+                    func=ACT.Exp,
+                    bias=neg_max[:, column : column + 1],
+                    scale=SCALE,
+                    accum_out=row_sum[:, column : column + 1],
+                )
+
+        def turn_e(h):
+            e_codes = e_mx_pool.tile([P, ROW_TILES, P], U32, align_bytes=64, name="e_codes")
+            e_scales = e_mx_pool.tile([P, ROW_TILES, P], U8, align_bytes=64, name="e_scales")
+            for pair in range(ROW_TILES // 2):
+                e_turned = et_ps.tile([P, 2, 2, P], F32, name="e_turned")
+                for cc in range(2):
+                    e_words = e_rows[h % 2][:, 2 * pair + cc, :].bitcast(F32)
+                    for u in range(2):
+                        nc.tensor.transpose(
+                            e_turned[:, cc, u, :], e_words[:, u * P : (u + 1) * P], ident_f32[:]
+                        )
+                e_grouped = stage.tile([P, 2 * P * PACK], BF16, align_bytes=64, name="e_grouped")
+                nc.scalar.copy(
+                    out=e_grouped[:].bitcast(F32).rearrange("p (c i u) -> p c i u", c=2, u=2),
+                    in_=e_turned[:].rearrange("p c u i -> p c i u"),
+                )
+                tiles = slice(2 * pair, 2 * pair + 2)
+                nc.vector.quantize_mx(
+                    out=e_codes[:, tiles, :].rearrange("p c i -> p (c i)").bitcast(FP8X4),
+                    scales=e_scales[:, tiles, :].rearrange("p c i -> p (c i)"),
+                    in_=e_grouped[:],
+                )
+            e_mx_of[h] = (e_codes, e_scales)
+
+        def project(h):
+            group, member = divmod(h, GROUP)
+            w_codes, w_scales = w_mx_of[group]
+            head_cols = slice(member * HD, (member + 1) * HD)
+            v_acc = v_ps.tile([P, ROW_TILES, HD], F32, name="v_acc")
+            for t in range(ROW_TILES):
+                for g in range(PASSES):
+                    nc.tensor.matmul_mx(
+                        out=v_acc[:, t, :],
+                        lhsT=x_codes[:, t, g, :].bitcast(FP8X4),
+                        lhsT_scale=x_scales[:, t, g, :],
+                        rhs=w_codes[:, g, head_cols].bitcast(FP8X4),
+                        rhs_scale=w_scales[:, g, head_cols],
+                        start=(g == 0),
+                        stop=(g == PASSES - 1),
+                    )
+            v_grouped = stage.tile([P, HD, PACK], BF16, align_bytes=64, name="v_grouped")
+            nc.vector.tensor_tensor(
+                out=v_grouped[:],
+                in0=v_acc[:].rearrange("m t d -> m d t"),
+                in1=bias_rows[:, h * HD : (h + 1) * HD].unsqueeze(2).to_broadcast([P, HD, PACK]),
+                op=ALU.add,
+            )
+            v_grouped_of[h] = v_grouped
+
+        def quantise_v(h):
+            v_codes = head_pool.tile([P, HD], U32, align_bytes=64, name="v_codes")
+            v_scales = head_pool.tile([P, HD], U8, align_bytes=64, name="v_scales")
+            nc.vector.quantize_mx(
+                out=v_codes[:].bitcast(FP8X4),
+                scales=v_scales[:],
+                in_=v_grouped_of[h][:].rearrange("m d t -> m (d t)"),
+            )
+            v_mx_of[h] = (v_codes, v_scales)
+
+        def attend(h):
+            e_codes, e_scales = e_mx_of[h]
+            v_codes, v_scales = v_mx_of[h]
+            ctx_acc = ctx_ps.tile([P, ROW_TILES, HD], F32, name="ctx_acc")
+            for c in range(ROW_TILES):
+                nc.tensor.matmul_mx(
+                    out=ctx_acc[:, c, :],
+                    lhsT=e_codes[:, c, :].bitcast(FP8X4),
+                    lhsT_scale=e_scales[:, c, :],
+                    rhs=v_codes[:].bitcast(FP8X4),
+                    rhs_scale=v_scales[:],
+                    start=True,
+                    stop=True,
+                )
+            columns = slice(h * ROW_TILES, (h + 1) * ROW_TILES)
+            nc.vector.reciprocal(out=inv_sum[:, columns], in_=row_sum[:, columns])
+            ctx_sb = head_pool.tile([P, ROW_TILES, HD], F32, name="ctx_sb")
+            nc.vector.tensor_tensor(
+                out=ctx_sb[:],
+                in0=ctx_acc[:],
+                in1=inv_sum[:, columns].unsqueeze(2).to_broadcast([P, ROW_TILES, HD]),
+                op=ALU.mult,
+            )
+            nc.sync.dma_start(out=out_rows[:, :, h * HD : (h + 1) * HD], in_=ctx_sb[:])
+
+        for h in range(TURN_QK_AHEAD):
+            turn_qk(h)
+        for step in range(STEPS):
+            if step + LOAD_QK_AHEAD < H:
+                load_qk(step + LOAD_QK_AHEAD)
+            if step % PASSES == 0 and step // PASSES + 1 < GROUPS:
+                load_chunk(step // PASSES + 1)
+            if 0 <= step - QUANTISE_W_LAG < W_PASSES:
+                quantise_w(step - QUANTISE_W_LAG)
+            if 0 <= step - TURN_E_LAG < H:
+                turn_e(step - TURN_E_LAG)
+            if 0 <= step - PROJECT_LAG < H:
+                project(step - PROJECT_LAG)
+            if 0 <= step - ATTEND_LAG < H:
+                attend(step - ATTEND_LAG)
+            if 0 <= step - PROJECT_LAG < H:
+                quantise_v(step - PROJECT_LAG)
+            if step + TURN_QK_AHEAD < H:
+                turn_qk(step + TURN_QK_AHEAD)
+            if 0 <= step - QUANTISE_W_LAG < ROW_TILES:
+                quantise_x(step - QUANTISE_W_LAG)
+            if step < H:
+                scores(step)
+            if step < W_PASSES:
+                regroup_w(step)

@@ -9,6 +9,7 @@ U8 = mybir.dt.uint8
 FP8X4 = mybir.dt.float8_e4m3fn_x4
 ALU = mybir.AluOpType
 ACT = mybir.ActivationFunctionType
+AXIS = mybir.AxisListType
 
 P = 128
 S = 512
@@ -39,14 +40,13 @@ def raw_slope(head):
     return 2.0 ** (-(head + 1) / 2.0) / SCALE
 
 
-TURN_QK_AHEAD = 1
-TURN_E_LAG = 2
-LOAD_QK_AHEAD = 3
-W_PASSES = GROUPS * PASSES
-QUANTISE_W_LAG = 1
-PROJECT_LAG = GROUP + QUANTISE_W_LAG
+LOAD_QK_AHEAD = 4
+X_START = 0
+REGROUP_LAG = 1
+PROJECT_LAG = REGROUP_LAG + 2
 ATTEND_LAG = PROJECT_LAG + 1
-STEPS = H + ATTEND_LAG
+HEAD_BUFS = 4
+STEPS = H + ATTEND_LAG + 1
 
 
 def tile_selfattention_pa_kernel(tc, x, Wv, bv, q, k, out):
@@ -54,12 +54,10 @@ def tile_selfattention_pa_kernel(tc, x, Wv, bv, q, k, out):
 
     with tc.tile_pool(name="consts", bufs=1) as consts, tc.tile_pool(
         name="fixed", bufs=1
-    ) as fixed, tc.tile_pool(name="w_raw", bufs=2) as w_raw_pool, tc.tile_pool(
-        name="w_mx", bufs=2
-    ) as w_mx_pool, tc.tile_pool(name="qk_raw", bufs=LOAD_QK_AHEAD + 1) as qk_raw_pool, tc.tile_pool(
+    ) as fixed, tc.tile_pool(name="w_raw", bufs=2) as w_raw_pool, tc.tile_pool(name="qk_raw", bufs=LOAD_QK_AHEAD + 1) as qk_raw_pool, tc.tile_pool(
         name="stage", bufs=3
-    ) as stage, tc.tile_pool(name="e_mx", bufs=ATTEND_LAG - TURN_E_LAG + 2) as e_mx_pool, tc.tile_pool(
-        name="head", bufs=3
+    ) as stage, tc.tile_pool(name="e_mx", bufs=ATTEND_LAG) as e_mx_pool, tc.tile_pool(
+        name="head", bufs=HEAD_BUFS
     ) as head_pool, tc.psum_pool(name="score_ps", bufs=1) as score_ps, tc.psum_pool(
         name="et_ps", bufs=2
     ) as et_ps, tc.psum_pool(name="turn_ps", bufs=1) as turn_ps, tc.psum_pool(
@@ -77,7 +75,13 @@ def tile_selfattention_pa_kernel(tc, x, Wv, bv, q, k, out):
         w_grouped_of = {}
         w_mx_of = {}
         e_mx_of = {}
+        qk_bank_of = {}
+        score_of_head = {}
+        e_bank_of = {}
+        e_grouped_of = {}
+        v_acc_of = {}
         v_grouped_of = {}
+        ctx_acc_of = {}
         v_mx_of = {}
 
         def load_qk(h):
@@ -94,47 +98,30 @@ def tile_selfattention_pa_kernel(tc, x, Wv, bv, q, k, out):
                 nc.sync.dma_start(out=w_raw[:, :, e, :], in_=w_rows[e, :, :, cols])
             w_raw_of[group] = w_raw
 
-        for h in range(LOAD_QK_AHEAD):
+        for h in range(3):
             load_qk(h)
-        load_chunk(0)
         x_sb = fixed.tile([P, ROW_TILES, D], BF16)
         for u in range(2):
             nc.sync.dma_start(
                 out=x_sb[:, 2 * u : 2 * u + 2, :].rearrange("m e k -> m (e k)"),
                 in_=x_rows[:, u, :],
             )
+        for h in range(3, LOAD_QK_AHEAD):
+            load_qk(h)
+        load_chunk(0)
         bias_rows = consts.tile([P, D], BF16)
         nc.sync.dma_start(out=bias_rows[:], in_=bv.partition_broadcast(P))
 
         ident_bf = consts.tile([P, P], BF16)
-        make_identity(nc, ident_bf[:])
-        ident_f32 = consts.tile([P, P], F32)
-        make_identity(nc, ident_f32[:])
-
-        bias_rhs = consts.tile([P, S], BF16)
-        nc.gpsimd.memset(bias_rhs[:MASK_ROWS, :], 0.0)
-        for odd, fill in ((0, MASK_EVEN), (1, MASK_ODD)):
-            nc.gpsimd.affine_select(
-                out=bias_rhs[:MASK_ROWS, :],
-                in_=bias_rhs[:MASK_ROWS, :],
-                compare_op=ALU.not_equal,
-                fill=fill,
-                base=-(S - P) - odd,
-                pattern=[[1, S]],
-                channel_multiplier=-2,
-            )
-        key_numbers = consts.tile([P, S], I32)
-        nc.gpsimd.iota(key_numbers[:], pattern=[[1, S]], base=-KEY_CENTRE, channel_multiplier=0)
-        nc.vector.tensor_scalar(
-            out=bias_rhs[MASK_ROWS:, :],
-            in0=key_numbers[MASK_ROWS:, :],
-            scalar1=1.0 / QUADRANT,
-            scalar2=None,
-            op0=ALU.mult,
-        )
-
         query_mask = consts.tile([P, P], F32)
-        nc.gpsimd.memset(query_mask[:], 1.0)
+        bias_rhs = consts.tile([P, S], BF16)
+        ident_f32 = consts.tile([P, P], F32)
+        nc.vector.memset(ident_bf[:], 0.0)
+        nc.vector.memset(query_mask[:], 1.0)
+        nc.vector.memset(bias_rhs[:MASK_ROWS, :], 0.0)
+        nc.vector.memset(ident_f32[:], 0.0)
+        make_identity(nc, ident_bf[:], nomemset=True)
+
         nc.gpsimd.affine_select(
             out=query_mask[:],
             in_=query_mask[:],
@@ -153,6 +140,19 @@ def tile_selfattention_pa_kernel(tc, x, Wv, bv, q, k, out):
             pattern=[[-1, P]],
             channel_multiplier=2,
         )
+        key_numbers = consts.tile([P, S], I32)
+        nc.gpsimd.iota(key_numbers[:], pattern=[[1, S]], base=-KEY_CENTRE, channel_multiplier=0)
+        for odd, fill in ((0, MASK_EVEN), (1, MASK_ODD)):
+            nc.gpsimd.affine_select(
+                out=bias_rhs[:MASK_ROWS, :],
+                in_=bias_rhs[:MASK_ROWS, :],
+                compare_op=ALU.not_equal,
+                fill=fill,
+                base=-(S - P) - odd,
+                pattern=[[1, S]],
+                channel_multiplier=-2,
+            )
+        make_identity(nc, ident_f32[:], nomemset=True)
 
         ones = consts.tile([P, 1], F32)
         nc.vector.memset(ones[:], 1.0)
@@ -167,10 +167,6 @@ def tile_selfattention_pa_kernel(tc, x, Wv, bv, q, k, out):
         nc.vector.tensor_tensor(out=slope_rest[:], in0=slope[:], in1=slope_high[:], op=ALU.subtract)
 
         bias_lhsT = consts.tile([P, H, P], BF16)
-        nc.vector.tensor_copy(
-            out=bias_lhsT[:MASK_ROWS, :, :],
-            in_=query_mask[:MASK_ROWS, :].unsqueeze(1).to_broadcast([MASK_ROWS, H, P]),
-        )
         high_rows = slice(MASK_ROWS, MASK_ROWS + QUADRANT)
         rest_rows = slice(MASK_ROWS + QUADRANT, P)
         nc.vector.tensor_copy(
@@ -181,11 +177,23 @@ def tile_selfattention_pa_kernel(tc, x, Wv, bv, q, k, out):
             out=bias_lhsT[rest_rows, :, :],
             in_=slope_rest[rest_rows, :].unsqueeze(2).to_broadcast([QUADRANT, H, P]),
         )
+        nc.scalar.copy(
+            out=bias_lhsT[:MASK_ROWS, :, :],
+            in_=query_mask[:MASK_ROWS, :].unsqueeze(1).to_broadcast([MASK_ROWS, H, P]),
+        )
+        nc.vector.tensor_scalar(
+            out=bias_rhs[MASK_ROWS:, :],
+            in0=key_numbers[MASK_ROWS:, :],
+            scalar1=1.0 / QUADRANT,
+            scalar2=None,
+            op0=ALU.mult,
+        )
 
         e_rows = [fixed.tile([P, ROW_TILES, S], BF16, name="e_rows%d" % par) for par in range(2)]
         for par in range(2):
             nc.vector.memset(e_rows[par][:].bitcast(I32), 0)
 
+        raw_max = fixed.tile([P, H * ROW_TILES], F32)
         neg_max = fixed.tile([P, H * ROW_TILES], F32)
         row_sum = fixed.tile([P, H * ROW_TILES], F32)
         inv_sum = fixed.tile([P, H * ROW_TILES], F32)
@@ -195,7 +203,10 @@ def tile_selfattention_pa_kernel(tc, x, Wv, bv, q, k, out):
         def quantise_x(t):
             x_words = x_sb[:, t, :].bitcast(F32)
             for half in range(2):
-                turned = turn_ps.tile([P, 4, P], F32, tag="turned")
+                if half == 0:
+                    turned = v_ps.tile([P, 4, P], F32, tag="v_acc")
+                else:
+                    turned = ctx_ps.tile([P, 4, P], F32, tag="ctx_acc")
                 for w in range(4):
                     plane = 4 * half + w
                     nc.tensor.transpose(
@@ -213,30 +224,27 @@ def tile_selfattention_pa_kernel(tc, x, Wv, bv, q, k, out):
                     in_=x_grouped[:],
                 )
 
-        def regroup_w(n):
-            group, g = divmod(n, PASSES)
-            w_grouped = stage.tile([P, CHUNK, PACK], BF16, align_bytes=64, name="w_grouped")
-            regroup = nc.scalar.copy if n % 2 else nc.vector.tensor_copy
-            regroup(
-                out=w_grouped[:].rearrange("p (c i) t -> p c t i", i=4),
-                in_=w_raw_of[group][:, 2 * g : 2 * g + 2, :, :]
-                .rearrange("p u e n -> p (u e) n")
-                .rearrange("p t (c i) -> p c t i", i=4),
+        def regroup_w(h):
+            group, member = divmod(h, GROUP)
+            head_cols = slice(member * HD, (member + 1) * HD)
+            w_grouped = stage.tile([P, PASSES, HD, PACK], BF16, align_bytes=64, name="w_grouped")
+            nc.vector.tensor_copy(
+                out=w_grouped[:].rearrange("p g (c i) t -> p g c t i", i=4),
+                in_=w_raw_of[group][:, :, :, head_cols]
+                .rearrange("p (g u) e n -> p g (u e) n", u=2)
+                .rearrange("p g t (c i) -> p g c t i", i=4),
             )
-            w_grouped_of[n] = w_grouped
+            w_grouped_of[h] = w_grouped
 
-        def quantise_w(n):
-            group, g = divmod(n, PASSES)
-            if g == 0:
-                w_codes = w_mx_pool.tile([P, PASSES, CHUNK], U32, align_bytes=64, name="w_codes")
-                w_scales = w_mx_pool.tile([P, PASSES, CHUNK], U8, align_bytes=64, name="w_scales")
-                w_mx_of[group] = (w_codes, w_scales)
-            w_codes, w_scales = w_mx_of[group]
+        def quantise_w(h):
+            w_codes = head_pool.tile([P, PASSES, HD], U32, align_bytes=64, name="w_codes")
+            w_scales = head_pool.tile([P, PASSES, HD], U8, align_bytes=64, name="w_scales")
             nc.vector.quantize_mx(
-                out=w_codes[:, g, :].bitcast(FP8X4),
-                scales=w_scales[:, g, :],
-                in_=w_grouped_of[n][:].rearrange("p n t -> p (n t)"),
+                out=w_codes[:].rearrange("p g n -> p (g n)").bitcast(FP8X4),
+                scales=w_scales[:].rearrange("p g n -> p (g n)"),
+                in_=w_grouped_of[h][:].rearrange("p g n t -> p (g n t)"),
             )
+            w_mx_of[h] = (w_codes, w_scales)
 
         def turn_qk(h):
             q_sb, k_sb = qk_sb[h]
@@ -244,8 +252,11 @@ def tile_selfattention_pa_kernel(tc, x, Wv, bv, q, k, out):
             for c in range(ROW_TILES):
                 nc.tensor.transpose(turned[:, c, :], q_sb[:, c, :], ident_bf[:])
                 nc.tensor.transpose(turned[:, ROW_TILES + c, :], k_sb[:, c, :], ident_bf[:])
+            qk_bank_of[h] = turned
+
+        def copy_qk(h):
             qk_t = head_pool.tile([P, 2 * ROW_TILES, P], BF16, name="qk_t")
-            nc.scalar.copy(out=qk_t[:], in_=turned[:])
+            nc.scalar.copy(out=qk_t[:], in_=qk_bank_of[h][:])
             qk_turned[h] = qk_t
 
         def scores(h):
@@ -275,22 +286,29 @@ def tile_selfattention_pa_kernel(tc, x, Wv, bv, q, k, out):
                     start=False,
                     stop=True,
                 )
+            score_of_head[h] = score_of
+
+        def row_maxima(h):
+            columns = slice(h * ROW_TILES, (h + 1) * ROW_TILES)
+            for c in range(ROW_TILES):
+                column = h * ROW_TILES + c
+                nc.vector.tensor_reduce(
+                    out=raw_max[:, column : column + 1],
+                    in_=score_of_head[h][c],
+                    axis=AXIS.X,
+                    op=ALU.max,
+                )
+            nc.vector.tensor_scalar(
+                out=neg_max[:, columns], in0=raw_max[:, columns], scalar1=-SCALE, scalar2=None, op0=ALU.mult
+            )
+
+        def exponentials(h):
             for c in range(ROW_TILES):
                 keys = (c + 1) * P
                 column = h * ROW_TILES + c
-                unused = stage.tile([P, S], BF16, name="unused")
-                nc.vector.tensor_scalar(
-                    out=unused[:, :keys],
-                    in0=score_of[c],
-                    scalar1=-SCALE,
-                    scalar2=None,
-                    op0=ALU.mult,
-                    op1=ALU.min,
-                    accum_out=neg_max[:, column : column + 1],
-                )
                 nc.scalar.activation(
                     out=e_rows[h % 2][:, c, :keys],
-                    in_=score_of[c],
+                    in_=score_of_head[h][c],
                     func=ACT.Exp,
                     bias=neg_max[:, column : column + 1],
                     scale=SCALE,
@@ -298,8 +316,7 @@ def tile_selfattention_pa_kernel(tc, x, Wv, bv, q, k, out):
                 )
 
         def turn_e(h):
-            e_codes = e_mx_pool.tile([P, ROW_TILES, P], U32, align_bytes=64, name="e_codes")
-            e_scales = e_mx_pool.tile([P, ROW_TILES, P], U8, align_bytes=64, name="e_scales")
+            e_bank_of[h] = []
             for pair in range(ROW_TILES // 2):
                 e_turned = et_ps.tile([P, 2, 2, P], F32, name="e_turned")
                 for cc in range(2):
@@ -308,23 +325,32 @@ def tile_selfattention_pa_kernel(tc, x, Wv, bv, q, k, out):
                         nc.tensor.transpose(
                             e_turned[:, cc, u, :], e_words[:, u * P : (u + 1) * P], ident_f32[:]
                         )
+                e_bank_of[h].append(e_turned)
+
+        def copy_e(h):
+            e_grouped_of[h] = []
+            for pair in range(ROW_TILES // 2):
                 e_grouped = stage.tile([P, 2 * P * PACK], BF16, align_bytes=64, name="e_grouped")
                 nc.scalar.copy(
                     out=e_grouped[:].bitcast(F32).rearrange("p (c i u) -> p c i u", c=2, u=2),
-                    in_=e_turned[:].rearrange("p c u i -> p c i u"),
+                    in_=e_bank_of[h][pair][:].rearrange("p c u i -> p c i u"),
                 )
+                e_grouped_of[h].append(e_grouped)
+
+        def quantise_e(h):
+            e_codes = e_mx_pool.tile([P, ROW_TILES, P], U32, align_bytes=64, name="e_codes")
+            e_scales = e_mx_pool.tile([P, ROW_TILES, P], U8, align_bytes=64, name="e_scales")
+            for pair in range(ROW_TILES // 2):
                 tiles = slice(2 * pair, 2 * pair + 2)
                 nc.vector.quantize_mx(
                     out=e_codes[:, tiles, :].rearrange("p c i -> p (c i)").bitcast(FP8X4),
                     scales=e_scales[:, tiles, :].rearrange("p c i -> p (c i)"),
-                    in_=e_grouped[:],
+                    in_=e_grouped_of[h][pair][:],
                 )
             e_mx_of[h] = (e_codes, e_scales)
 
         def project(h):
-            group, member = divmod(h, GROUP)
-            w_codes, w_scales = w_mx_of[group]
-            head_cols = slice(member * HD, (member + 1) * HD)
+            w_codes, w_scales = w_mx_of[h]
             v_acc = v_ps.tile([P, ROW_TILES, HD], F32, name="v_acc")
             for t in range(ROW_TILES):
                 for g in range(PASSES):
@@ -332,15 +358,18 @@ def tile_selfattention_pa_kernel(tc, x, Wv, bv, q, k, out):
                         out=v_acc[:, t, :],
                         lhsT=x_codes[:, t, g, :].bitcast(FP8X4),
                         lhsT_scale=x_scales[:, t, g, :],
-                        rhs=w_codes[:, g, head_cols].bitcast(FP8X4),
-                        rhs_scale=w_scales[:, g, head_cols],
+                        rhs=w_codes[:, g, :].bitcast(FP8X4),
+                        rhs_scale=w_scales[:, g, :],
                         start=(g == 0),
                         stop=(g == PASSES - 1),
                     )
+            v_acc_of[h] = v_acc
+
+        def add_bias(h):
             v_grouped = stage.tile([P, HD, PACK], BF16, align_bytes=64, name="v_grouped")
             nc.vector.tensor_tensor(
                 out=v_grouped[:],
-                in0=v_acc[:].rearrange("m t d -> m d t"),
+                in0=v_acc_of[h][:].rearrange("m t d -> m d t"),
                 in1=bias_rows[:, h * HD : (h + 1) * HD].unsqueeze(2).to_broadcast([P, HD, PACK]),
                 op=ALU.add,
             )
@@ -370,39 +399,67 @@ def tile_selfattention_pa_kernel(tc, x, Wv, bv, q, k, out):
                     start=True,
                     stop=True,
                 )
+            ctx_acc_of[h] = ctx_acc
+
+        def invert_sums(h):
             columns = slice(h * ROW_TILES, (h + 1) * ROW_TILES)
             nc.vector.reciprocal(out=inv_sum[:, columns], in_=row_sum[:, columns])
+
+        def normalise(h):
             ctx_sb = head_pool.tile([P, ROW_TILES, HD], F32, name="ctx_sb")
-            nc.vector.tensor_tensor(
-                out=ctx_sb[:],
-                in0=ctx_acc[:],
-                in1=inv_sum[:, columns].unsqueeze(2).to_broadcast([P, ROW_TILES, HD]),
-                op=ALU.mult,
-            )
+            for c in range(ROW_TILES):
+                column = h * ROW_TILES + c
+                nc.scalar.activation(
+                    out=ctx_sb[:, c, :],
+                    in_=ctx_acc_of[h][:, c, :],
+                    func=ACT.Copy,
+                    scale=inv_sum[:, column : column + 1],
+                )
             nc.sync.dma_start(out=out_rows[:, :, h * HD : (h + 1) * HD], in_=ctx_sb[:])
 
-        for h in range(TURN_QK_AHEAD):
-            turn_qk(h)
+        def in_range(index, count):
+            return 0 <= index < count
+
+        turn_qk(0)
+        copy_qk(0)
+        turn_qk(1)
+        scores(0)
         for step in range(STEPS):
-            if step + LOAD_QK_AHEAD < H:
+            if in_range(step + LOAD_QK_AHEAD, H):
                 load_qk(step + LOAD_QK_AHEAD)
-            if step % PASSES == 0 and step // PASSES + 1 < GROUPS:
-                load_chunk(step // PASSES + 1)
-            if 0 <= step - QUANTISE_W_LAG < W_PASSES:
-                quantise_w(step - QUANTISE_W_LAG)
-            if 0 <= step - TURN_E_LAG < H:
-                turn_e(step - TURN_E_LAG)
-            if 0 <= step - PROJECT_LAG < H:
+            if (step - REGROUP_LAG) % GROUP == 0 and in_range((step - REGROUP_LAG) // GROUP + 1, GROUPS):
+                load_chunk((step - REGROUP_LAG) // GROUP + 1)
+            if in_range(step, H):
+                row_maxima(step)
+            if in_range(step - 2, H):
+                copy_e(step - 2)
+            if in_range(step + 1, H):
+                copy_qk(step + 1)
+            if in_range(step, H):
+                exponentials(step)
+            if in_range(step - ATTEND_LAG, H):
+                invert_sums(step - ATTEND_LAG)
+            if in_range(step - 2, H):
+                quantise_e(step - 2)
+            if in_range(step - PROJECT_LAG, H):
                 project(step - PROJECT_LAG)
-            if 0 <= step - ATTEND_LAG < H:
+            if in_range(step - ATTEND_LAG, H):
                 attend(step - ATTEND_LAG)
-            if 0 <= step - PROJECT_LAG < H:
+                normalise(step - ATTEND_LAG)
+            if in_range(step - PROJECT_LAG, H):
+                add_bias(step - PROJECT_LAG)
+            if in_range(step - X_START, 2):
+                quantise_x(2 * (step - X_START))
+                quantise_x(2 * (step - X_START) + 1)
+            if in_range(step - REGROUP_LAG, H):
+                regroup_w(step - REGROUP_LAG)
+            if in_range(step - REGROUP_LAG - 1, H):
+                quantise_w(step - REGROUP_LAG - 1)
+            if in_range(step - PROJECT_LAG, H):
                 quantise_v(step - PROJECT_LAG)
-            if step + TURN_QK_AHEAD < H:
-                turn_qk(step + TURN_QK_AHEAD)
-            if 0 <= step - QUANTISE_W_LAG < ROW_TILES:
-                quantise_x(step - QUANTISE_W_LAG)
-            if step < H:
-                scores(step)
-            if step < W_PASSES:
-                regroup_w(step)
+            if in_range(step - 1, H):
+                turn_e(step - 1)
+            if in_range(step + 2, H):
+                turn_qk(step + 2)
+            if in_range(step + 1, H):
+                scores(step + 1)

@@ -62,7 +62,7 @@ def tile_selfattention_pa_kernel(tc, x, Wv, bv, q, k, out):
         name="et_ps", bufs=2
     ) as et_ps, tc.psum_pool(name="turn_ps", bufs=1) as turn_ps, tc.psum_pool(
         name="v_ps", bufs=1
-    ) as v_ps, tc.psum_pool(name="ctx_ps", bufs=1) as ctx_ps, tc.manual_schedule():
+    ) as v_ps, tc.psum_pool(name="ctx_ps", bufs=1) as ctx_ps:
         q_rows = q.rearrange("b h (c p) d -> p (b h) c d", p=P)
         k_rows = k.rearrange("b h (c p) d -> p (b h) c d", p=P)
         w_rows = Wv.rearrange("(l p e) n -> e p l n", l=PLANES, e=2)

@@ -48,6 +48,13 @@ ATTEND_LAG = PROJECT_LAG + 1
 HEAD_BUFS = 4
 STEPS = H + ATTEND_LAG + 1
 
+TILE_KEYS = sum((c + 1) * P for c in range(ROW_TILES))
+
+
+def key_columns(c):
+    start = sum((b + 1) * P for b in range(c))
+    return slice(start, start + (c + 1) * P)
+
 
 def tile_selfattention_pa_kernel(tc, x, Wv, bv, q, k, out):
     nc = tc.nc
@@ -56,7 +63,7 @@ def tile_selfattention_pa_kernel(tc, x, Wv, bv, q, k, out):
         name="fixed", bufs=1
     ) as fixed, tc.tile_pool(name="w_raw", bufs=2) as w_raw_pool, tc.tile_pool(name="qk_raw", bufs=LOAD_QK_AHEAD + 1) as qk_raw_pool, tc.tile_pool(
         name="stage", bufs=3
-    ) as stage, tc.tile_pool(name="e_mx", bufs=ATTEND_LAG) as e_mx_pool, tc.tile_pool(
+    ) as stage, tc.tile_pool(name="scaled", bufs=2) as scaled_pool, tc.tile_pool(name="e_mx", bufs=ATTEND_LAG) as e_mx_pool, tc.tile_pool(
         name="head", bufs=HEAD_BUFS
     ) as head_pool, tc.psum_pool(name="score_ps", bufs=1) as score_ps, tc.psum_pool(
         name="et_ps", bufs=2
@@ -77,6 +84,7 @@ def tile_selfattention_pa_kernel(tc, x, Wv, bv, q, k, out):
         e_mx_of = {}
         qk_bank_of = {}
         score_of_head = {}
+        scaled_of = {}
         e_bank_of = {}
         e_grouped_of = {}
         v_acc_of = {}
@@ -193,7 +201,6 @@ def tile_selfattention_pa_kernel(tc, x, Wv, bv, q, k, out):
         for par in range(2):
             nc.vector.memset(e_rows[par][:].bitcast(I32), 0)
 
-        raw_max = fixed.tile([P, H * ROW_TILES], F32)
         neg_max = fixed.tile([P, H * ROW_TILES], F32)
         row_sum = fixed.tile([P, H * ROW_TILES], F32)
         inv_sum = fixed.tile([P, H * ROW_TILES], F32)
@@ -289,18 +296,19 @@ def tile_selfattention_pa_kernel(tc, x, Wv, bv, q, k, out):
             score_of_head[h] = score_of
 
         def row_maxima(h):
-            columns = slice(h * ROW_TILES, (h + 1) * ROW_TILES)
+            scaled = scaled_pool.tile([P, TILE_KEYS], F32, name="scaled")
             for c in range(ROW_TILES):
                 column = h * ROW_TILES + c
-                nc.vector.tensor_reduce(
-                    out=raw_max[:, column : column + 1],
-                    in_=score_of_head[h][c],
-                    axis=AXIS.X,
-                    op=ALU.max,
+                nc.vector.tensor_scalar(
+                    out=scaled[:, key_columns(c)],
+                    in0=score_of_head[h][c],
+                    scalar1=-SCALE,
+                    scalar2=None,
+                    op0=ALU.mult,
+                    op1=ALU.min,
+                    accum_out=neg_max[:, column : column + 1],
                 )
-            nc.vector.tensor_scalar(
-                out=neg_max[:, columns], in0=raw_max[:, columns], scalar1=-SCALE, scalar2=None, op0=ALU.mult
-            )
+            scaled_of[h] = scaled
 
         def exponentials(h):
             for c in range(ROW_TILES):
@@ -308,10 +316,10 @@ def tile_selfattention_pa_kernel(tc, x, Wv, bv, q, k, out):
                 column = h * ROW_TILES + c
                 nc.scalar.activation(
                     out=e_rows[h % 2][:, c, :keys],
-                    in_=score_of_head[h][c],
+                    in_=scaled_of[h][:, key_columns(c)],
                     func=ACT.Exp,
                     bias=neg_max[:, column : column + 1],
-                    scale=SCALE,
+                    scale=-1.0,
                     accum_out=row_sum[:, column : column + 1],
                 )
 

@@ -1,3 +1,5 @@
+from contextlib import ExitStack
+
 import concourse.mybir as mybir
 from concourse.masks import make_identity
 
@@ -9,7 +11,6 @@ U8 = mybir.dt.uint8
 FP8X4 = mybir.dt.float8_e4m3fn_x4
 ALU = mybir.AluOpType
 ACT = mybir.ActivationFunctionType
-AXIS = mybir.AxisListType
 
 P = 128
 S = 512
@@ -36,17 +37,11 @@ MASK_ODD = -(2.0**126)
 FLOPS = 2 * S * D * D + 2 * 2 * H * S * S * HD
 
 
-def raw_slope(head):
-    return 2.0 ** (-(head + 1) / 2.0) / SCALE
-
-
-LOAD_QK_AHEAD = 4
-X_START = 0
-REGROUP_LAG = 1
-PROJECT_LAG = REGROUP_LAG + 2
+TURN_QK_AHEAD = 2
+QUANTISE_W_LAG = 1
+PROJECT_LAG = 3
 ATTEND_LAG = PROJECT_LAG + 1
-HEAD_BUFS = 4
-STEPS = H + ATTEND_LAG + 1
+GPSIMD_PASSES = 2
 
 TILE_KEYS = sum((c + 1) * P for c in range(ROW_TILES))
 
@@ -59,17 +54,23 @@ def key_columns(c):
 def tile_selfattention_pa_kernel(tc, x, Wv, bv, q, k, out):
     nc = tc.nc
 
-    with tc.tile_pool(name="consts", bufs=1) as consts, tc.tile_pool(
-        name="fixed", bufs=1
-    ) as fixed, tc.tile_pool(name="w_raw", bufs=2) as w_raw_pool, tc.tile_pool(name="qk_raw", bufs=LOAD_QK_AHEAD + 1) as qk_raw_pool, tc.tile_pool(
-        name="stage", bufs=3
-    ) as stage, tc.tile_pool(name="scaled", bufs=2) as scaled_pool, tc.tile_pool(name="e_mx", bufs=ATTEND_LAG) as e_mx_pool, tc.tile_pool(
-        name="head", bufs=HEAD_BUFS
-    ) as head_pool, tc.psum_pool(name="score_ps", bufs=1) as score_ps, tc.psum_pool(
-        name="et_ps", bufs=2
-    ) as et_ps, tc.psum_pool(name="turn_ps", bufs=1) as turn_ps, tc.psum_pool(
-        name="v_ps", bufs=1
-    ) as v_ps, tc.psum_pool(name="ctx_ps", bufs=1) as ctx_ps:
+    with ExitStack() as ctx:
+        consts = ctx.enter_context(tc.tile_pool(name="consts", bufs=1))
+        fixed = ctx.enter_context(tc.tile_pool(name="fixed", bufs=1))
+        w_raw_pool = ctx.enter_context(tc.tile_pool(name="w_raw", bufs=GROUPS))
+        qk_raw_pool = ctx.enter_context(tc.tile_pool(name="qk_raw", bufs=H))
+        stage = ctx.enter_context(tc.tile_pool(name="stage", bufs=2))
+        x_stage = ctx.enter_context(tc.tile_pool(name="x_stage", bufs=4))
+        w_stage = ctx.enter_context(tc.tile_pool(name="w_stage", bufs=1))
+        scaled_pool = ctx.enter_context(tc.tile_pool(name="scaled", bufs=2))
+        e_mx_pool = ctx.enter_context(tc.tile_pool(name="e_mx", bufs=ATTEND_LAG))
+        w_mx_pool = ctx.enter_context(tc.tile_pool(name="w_mx", bufs=3))
+        out_pool = ctx.enter_context(tc.tile_pool(name="out", bufs=4))
+        head_pool = ctx.enter_context(tc.tile_pool(name="head", bufs=2))
+        score_ps = ctx.enter_context(tc.psum_pool(name="score_ps", bufs=1))
+        turn_ps = ctx.enter_context(tc.psum_pool(name="turn_ps", bufs=1))
+        mx_ps = ctx.enter_context(tc.psum_pool(name="mx_ps", bufs=1))
+
         q_rows = q.rearrange("b h (c p) d -> p (b h) c d", p=P)
         k_rows = k.rearrange("b h (c p) d -> p (b h) c d", p=P)
         w_rows = Wv.rearrange("(l p e) n -> e p l n", l=PLANES, e=2)
@@ -106,19 +107,25 @@ def tile_selfattention_pa_kernel(tc, x, Wv, bv, q, k, out):
                 nc.sync.dma_start(out=w_raw[:, :, e, :], in_=w_rows[e, :, :, cols])
             w_raw_of[group] = w_raw
 
-        for h in range(3):
-            load_qk(h)
         x_sb = fixed.tile([P, ROW_TILES, D], BF16)
-        for u in range(2):
-            nc.sync.dma_start(
-                out=x_sb[:, 2 * u : 2 * u + 2, :].rearrange("m e k -> m (e k)"),
-                in_=x_rows[:, u, :],
-            )
-        for h in range(3, LOAD_QK_AHEAD):
-            load_qk(h)
-        load_chunk(0)
         bias_rows = consts.tile([P, D], BF16)
-        nc.sync.dma_start(out=bias_rows[:], in_=bv.partition_broadcast(P))
+        with tc.manual_schedule(engines={mybir.EngineType.SP}):
+            load_qk(0)
+            load_qk(1)
+            for u in range(2):
+                nc.sync.dma_start(
+                    out=x_sb[:, 2 * u : 2 * u + 2, :].rearrange("m e k -> m (e k)"),
+                    in_=x_rows[:, u, :],
+                )
+                load_qk(2 + u)
+            load_chunk(0)
+            for h in range(4, 7):
+                load_qk(h)
+            nc.sync.dma_start(out=bias_rows[:], in_=bv.partition_broadcast(P))
+            for group in range(1, GROUPS):
+                load_chunk(group)
+                for h in range(GROUP * group + 3, min(GROUP * group + 7, H)):
+                    load_qk(h)
 
         ident_bf = consts.tile([P, P], BF16)
         query_mask = consts.tile([P, P], F32)
@@ -162,17 +169,17 @@ def tile_selfattention_pa_kernel(tc, x, Wv, bv, q, k, out):
             )
         make_identity(nc, ident_f32[:], nomemset=True)
 
-        ones = consts.tile([P, 1], F32)
-        nc.vector.memset(ones[:], 1.0)
-        slope = consts.tile([P, H], F32)
-        for h in range(H):
-            nc.vector.tensor_scalar(
-                out=slope[:, h : h + 1], in0=ones[:], scalar1=raw_slope(h), scalar2=None, op0=ALU.mult
-            )
+        slope = consts.tile([P, H // 2, 2], F32)
+        for n in range(H // 2):
+            nc.vector.memset(slope[:, n, :], 2.0 ** (3 - n))
+        nc.vector.tensor_scalar(
+            out=slope[:, :, 1], in0=slope[:, :, 1], scalar1=2.0**-0.5, scalar2=None, op0=ALU.mult
+        )
+        slope = slope[:].rearrange("p n i -> p (n i)")
         slope_high = consts.tile([P, H], BF16)
-        nc.vector.tensor_copy(out=slope_high[:], in_=slope[:])
+        nc.vector.tensor_copy(out=slope_high[:], in_=slope)
         slope_rest = consts.tile([P, H], F32)
-        nc.vector.tensor_tensor(out=slope_rest[:], in0=slope[:], in1=slope_high[:], op=ALU.subtract)
+        nc.vector.tensor_tensor(out=slope_rest[:], in0=slope, in1=slope_high[:], op=ALU.subtract)
 
         bias_lhsT = consts.tile([P, H, P], BF16)
         high_rows = slice(MASK_ROWS, MASK_ROWS + QUADRANT)
@@ -199,53 +206,79 @@ def tile_selfattention_pa_kernel(tc, x, Wv, bv, q, k, out):
 
         e_rows = [fixed.tile([P, ROW_TILES, S], BF16, name="e_rows%d" % par) for par in range(2)]
         for par in range(2):
-            nc.vector.memset(e_rows[par][:].bitcast(I32), 0)
+            for c in (0, 2):
+                nc.gpsimd.memset(e_rows[par][:, c, (c + 1) * P : (c + 2) * P], 0.0)
+        zeros = consts.tile([P, P], F32)
+        nc.gpsimd.memset(zeros[:], 0.0)
+        e_low = turn_ps.tile([P, 2, 2, P], F32, name="e_low")
+        exp_probe = consts.tile([P, 1], F32)
+        nc.scalar.activation(out=exp_probe[:], in_=ident_f32[:, :1], func=ACT.Exp)
 
         neg_max = fixed.tile([P, H * ROW_TILES], F32)
         row_sum = fixed.tile([P, H * ROW_TILES], F32)
         inv_sum = fixed.tile([P, H * ROW_TILES], F32)
+        x_bank_of = {}
+        x_grouped_of = {}
         x_codes = fixed.tile([P, ROW_TILES, PASSES, P], U32, align_bytes=64)
         x_scales = fixed.tile([P, ROW_TILES, PASSES, P], U8, align_bytes=64)
 
-        def quantise_x(t):
+        def turn_x(unit):
+            t, half = divmod(unit, 2)
             x_words = x_sb[:, t, :].bitcast(F32)
-            for half in range(2):
-                if half == 0:
-                    turned = v_ps.tile([P, 4, P], F32, tag="v_acc")
-                else:
-                    turned = ctx_ps.tile([P, 4, P], F32, tag="ctx_acc")
-                for w in range(4):
-                    plane = 4 * half + w
-                    nc.tensor.transpose(
-                        turned[:, w, :], x_words[:, plane * P : (plane + 1) * P], ident_f32[:]
-                    )
-                x_grouped = stage.tile([P, 2 * P * PACK], BF16, align_bytes=64)
-                nc.scalar.copy(
-                    out=x_grouped[:].bitcast(F32).rearrange("p (g m u) -> p g m u", g=2, u=2),
-                    in_=turned[:].rearrange("p (g u) m -> p g m u", u=2),
+            turned = mx_ps.tile([P, 4, P], F32, name="x_turned", tag=("v", "ctx")[half])
+            for w in range(4):
+                plane = 4 * half + w
+                nc.tensor.transpose(
+                    turned[:, w, :], x_words[:, plane * P : (plane + 1) * P], ident_f32[:]
                 )
-                passes = slice(2 * half, 2 * half + 2)
-                nc.vector.quantize_mx(
-                    out=x_codes[:, t, passes, :].rearrange("p g m -> p (g m)").bitcast(FP8X4),
-                    scales=x_scales[:, t, passes, :].rearrange("p g m -> p (g m)"),
-                    in_=x_grouped[:],
-                )
+            x_bank_of[unit] = turned
 
-        def regroup_w(h):
+        def copy_x(unit):
+            x_grouped = x_stage.tile([P, 2 * P * PACK], BF16, align_bytes=64, name="x_grouped")
+            copy = nc.scalar.copy if unit % 2 == 0 else nc.vector.tensor_copy
+            copy(
+                out=x_grouped[:].bitcast(F32).rearrange("p (g m u) -> p g m u", g=2, u=2),
+                in_=x_bank_of[unit][:].rearrange("p (g u) m -> p g m u", u=2),
+            )
+            x_grouped_of[unit] = x_grouped
+
+        def quantise_x(unit):
+            t, half = divmod(unit, 2)
+            passes = slice(2 * half, 2 * half + 2)
+            nc.vector.quantize_mx(
+                out=x_codes[:, t, passes, :].rearrange("p g m -> p (g m)").bitcast(FP8X4),
+                scales=x_scales[:, t, passes, :].rearrange("p g m -> p (g m)"),
+                in_=x_grouped_of[unit][:],
+            )
+
+        def regroup_w(h, engine):
             group, member = divmod(h, GROUP)
             head_cols = slice(member * HD, (member + 1) * HD)
-            w_grouped = stage.tile([P, PASSES, HD, PACK], BF16, align_bytes=64, name="w_grouped")
-            nc.vector.tensor_copy(
-                out=w_grouped[:].rearrange("p g (c i) t -> p g c t i", i=4),
-                in_=w_raw_of[group][:, :, :, head_cols]
-                .rearrange("p (g u) e n -> p g (u e) n", u=2)
-                .rearrange("p g t (c i) -> p g c t i", i=4),
+            rows_of_pass = w_raw_of[group][:, :, :, head_cols].rearrange(
+                "p (g u) e n -> p g (u e) n", u=2
             )
-            w_grouped_of[h] = w_grouped
+            if engine == "gpsimd":
+                w_grouped = w_stage.tile([P, PASSES, HD, PACK], BF16, align_bytes=64, name="w_grouped")
+                w_grouped_of[h] = w_grouped
+                nc.gpsimd.tensor_scalar(
+                    out=w_grouped[:, :GPSIMD_PASSES, :, :],
+                    in0=rows_of_pass[:, :GPSIMD_PASSES, :, :].rearrange("p g t n -> p g n t"),
+                    scalar1=1.0,
+                    scalar2=0.0,
+                    op0=ALU.mult,
+                    op1=ALU.add,
+                )
+            else:
+                nc.vector.tensor_copy(
+                    out=w_grouped_of[h][:, GPSIMD_PASSES:, :, :].rearrange(
+                        "p g (c i) t -> p g c t i", i=4
+                    ),
+                    in_=rows_of_pass[:, GPSIMD_PASSES:, :, :].rearrange("p g t (c i) -> p g c t i", i=4),
+                )
 
         def quantise_w(h):
-            w_codes = head_pool.tile([P, PASSES, HD], U32, align_bytes=64, name="w_codes")
-            w_scales = head_pool.tile([P, PASSES, HD], U8, align_bytes=64, name="w_scales")
+            w_codes = w_mx_pool.tile([P, PASSES, HD], U32, align_bytes=64, name="w_codes")
+            w_scales = w_mx_pool.tile([P, PASSES, HD], U8, align_bytes=64, name="w_scales")
             nc.vector.quantize_mx(
                 out=w_codes[:].rearrange("p g n -> p (g n)").bitcast(FP8X4),
                 scales=w_scales[:].rearrange("p g n -> p (g n)"),
@@ -255,7 +288,7 @@ def tile_selfattention_pa_kernel(tc, x, Wv, bv, q, k, out):
 
         def turn_qk(h):
             q_sb, k_sb = qk_sb[h]
-            turned = turn_ps.tile([P, 2 * ROW_TILES, P], BF16, tag="turned")
+            turned = turn_ps.tile([P, 2 * ROW_TILES, P], BF16, name="qk_bank")
             for c in range(ROW_TILES):
                 nc.tensor.transpose(turned[:, c, :], q_sb[:, c, :], ident_bf[:])
                 nc.tensor.transpose(turned[:, ROW_TILES + c, :], k_sb[:, c, :], ident_bf[:])
@@ -323,43 +356,46 @@ def tile_selfattention_pa_kernel(tc, x, Wv, bv, q, k, out):
                     accum_out=row_sum[:, column : column + 1],
                 )
 
-        def turn_e(h):
-            e_bank_of[h] = []
-            for pair in range(ROW_TILES // 2):
-                e_turned = et_ps.tile([P, 2, 2, P], F32, name="e_turned")
-                for cc in range(2):
-                    e_words = e_rows[h % 2][:, 2 * pair + cc, :].bitcast(F32)
-                    for u in range(2):
-                        nc.tensor.transpose(
-                            e_turned[:, cc, u, :], e_words[:, u * P : (u + 1) * P], ident_f32[:]
-                        )
-                e_bank_of[h].append(e_turned)
+        def turn_e(h, pair):
+            if pair == 0:
+                turned = e_low
+            else:
+                turned = turn_ps.tile([P, 2, 2, P], F32, name="e_high")
+            for cc in range(2):
+                e_words = e_rows[h % 2][:, 2 * pair + cc, :].bitcast(F32)
+                for u in range(pair + 1):
+                    nc.tensor.transpose(
+                        turned[:, cc, u, :], e_words[:, u * P : (u + 1) * P], ident_f32[:]
+                    )
+            e_bank_of[h, pair] = turned
 
-        def copy_e(h):
-            e_grouped_of[h] = []
-            for pair in range(ROW_TILES // 2):
-                e_grouped = stage.tile([P, 2 * P * PACK], BF16, align_bytes=64, name="e_grouped")
-                nc.scalar.copy(
-                    out=e_grouped[:].bitcast(F32).rearrange("p (c i u) -> p c i u", c=2, u=2),
-                    in_=e_bank_of[h][pair][:].rearrange("p c u i -> p c i u"),
-                )
-                e_grouped_of[h].append(e_grouped)
+        def copy_e(h, pair):
+            e_grouped = stage.tile(
+                [P, 2 * P * PACK], BF16, align_bytes=64, name=("e_grouped_low", "e_grouped_high")[pair]
+            )
+            copy = nc.vector.tensor_copy if h >= H - 2 and pair == 1 else nc.scalar.copy
+            copy(
+                out=e_grouped[:].bitcast(F32).rearrange("p (c i u) -> p c i u", c=2, u=2),
+                in_=e_bank_of[h, pair][:].rearrange("p c u i -> p c i u"),
+            )
+            e_grouped_of[h, pair] = e_grouped
 
-        def quantise_e(h):
-            e_codes = e_mx_pool.tile([P, ROW_TILES, P], U32, align_bytes=64, name="e_codes")
-            e_scales = e_mx_pool.tile([P, ROW_TILES, P], U8, align_bytes=64, name="e_scales")
-            for pair in range(ROW_TILES // 2):
-                tiles = slice(2 * pair, 2 * pair + 2)
-                nc.vector.quantize_mx(
-                    out=e_codes[:, tiles, :].rearrange("p c i -> p (c i)").bitcast(FP8X4),
-                    scales=e_scales[:, tiles, :].rearrange("p c i -> p (c i)"),
-                    in_=e_grouped_of[h][pair][:],
-                )
-            e_mx_of[h] = (e_codes, e_scales)
+        def quantise_e(h, pair):
+            if pair == 0:
+                e_codes = e_mx_pool.tile([P, ROW_TILES, P], U32, align_bytes=64, name="e_codes")
+                e_scales = e_mx_pool.tile([P, ROW_TILES, P], U8, align_bytes=64, name="e_scales")
+                e_mx_of[h] = (e_codes, e_scales)
+            e_codes, e_scales = e_mx_of[h]
+            tiles = slice(2 * pair, 2 * pair + 2)
+            nc.vector.quantize_mx(
+                out=e_codes[:, tiles, :].rearrange("p c i -> p (c i)").bitcast(FP8X4),
+                scales=e_scales[:, tiles, :].rearrange("p c i -> p (c i)"),
+                in_=e_grouped_of[h, pair][:],
+            )
 
-        def project(h):
+        def project(h, pool, bank):
             w_codes, w_scales = w_mx_of[h]
-            v_acc = v_ps.tile([P, ROW_TILES, HD], F32, name="v_acc")
+            v_acc = pool.tile([P, ROW_TILES, HD], F32, name="v_acc", tag=bank)
             for t in range(ROW_TILES):
                 for g in range(PASSES):
                     nc.tensor.matmul_mx(
@@ -393,10 +429,10 @@ def tile_selfattention_pa_kernel(tc, x, Wv, bv, q, k, out):
             )
             v_mx_of[h] = (v_codes, v_scales)
 
-        def attend(h):
+        def attend(h, pool, bank):
             e_codes, e_scales = e_mx_of[h]
             v_codes, v_scales = v_mx_of[h]
-            ctx_acc = ctx_ps.tile([P, ROW_TILES, HD], F32, name="ctx_acc")
+            ctx_acc = pool.tile([P, ROW_TILES, HD], F32, name="ctx_acc", tag=bank)
             for c in range(ROW_TILES):
                 nc.tensor.matmul_mx(
                     out=ctx_acc[:, c, :],
@@ -413,9 +449,18 @@ def tile_selfattention_pa_kernel(tc, x, Wv, bv, q, k, out):
             columns = slice(h * ROW_TILES, (h + 1) * ROW_TILES)
             nc.vector.reciprocal(out=inv_sum[:, columns], in_=row_sum[:, columns])
 
-        def normalise(h):
-            ctx_sb = head_pool.tile([P, ROW_TILES, HD], F32, name="ctx_sb")
-            for c in range(ROW_TILES):
+        def normalise(h, on_scalar=ROW_TILES):
+            ctx_sb = out_pool.tile([P, ROW_TILES, HD], F32, name="ctx_sb")
+            if on_scalar < ROW_TILES:
+                rest = slice(on_scalar, ROW_TILES)
+                inverse = inv_sum[:, h * ROW_TILES + on_scalar : (h + 1) * ROW_TILES]
+                nc.vector.tensor_tensor(
+                    out=ctx_sb[:, rest, :],
+                    in0=ctx_acc_of[h][:, rest, :],
+                    in1=inverse.unsqueeze(2).to_broadcast([P, ROW_TILES - on_scalar, HD]),
+                    op=ALU.mult,
+                )
+            for c in range(on_scalar):
                 column = h * ROW_TILES + c
                 nc.scalar.activation(
                     out=ctx_sb[:, c, :],
@@ -425,49 +470,86 @@ def tile_selfattention_pa_kernel(tc, x, Wv, bv, q, k, out):
                 )
             nc.sync.dma_start(out=out_rows[:, :, h * HD : (h + 1) * HD], in_=ctx_sb[:])
 
-        def in_range(index, count):
-            return 0 <= index < count
+        def with_head(stage_of_head, h, *args):
+            if 0 <= h < H:
+                stage_of_head(h, *args)
 
-        turn_qk(0)
-        copy_qk(0)
-        turn_qk(1)
-        scores(0)
-        for step in range(STEPS):
-            if in_range(step + LOAD_QK_AHEAD, H):
-                load_qk(step + LOAD_QK_AHEAD)
-            if (step - REGROUP_LAG) % GROUP == 0 and in_range((step - REGROUP_LAG) // GROUP + 1, GROUPS):
-                load_chunk((step - REGROUP_LAG) // GROUP + 1)
-            if in_range(step, H):
+        x_first = {1: (2, 3), 2: (6, 7)}
+        x_last = {0: (0, 1), 1: (4, 5)}
+
+        with tc.manual_schedule():
+            turn_qk(0)
+            copy_qk(0)
+            turn_qk(1)
+            for cc in range(2):
+                nc.tensor.transpose(e_low[:, cc, 1, :], zeros[:], ident_f32[:])
+            scores(0)
+            for step in range(H):
+                weight_head = step - QUANTISE_W_LAG
+                project_head = step - PROJECT_LAG
+                attend_head = step - ATTEND_LAG
+                late_units = x_last.get(step - 1, ())
+                units = x_first.get(step, ())
+                for unit in late_units:
+                    copy_x(unit)
+                with_head(invert_sums, attend_head)
+                with_head(project, project_head, mx_ps, "v")
+                with_head(attend, attend_head, mx_ps, "ctx")
+                for unit in units:
+                    turn_x(unit)
+                with_head(copy_qk, step + 1)
+                with_head(copy_e, step - 2, 0)
+                with_head(copy_e, step - 2, 1)
                 row_maxima(step)
-            if in_range(step - 2, H):
-                copy_e(step - 2)
-            if in_range(step + 1, H):
-                copy_qk(step + 1)
-            if in_range(step, H):
+                with_head(add_bias, project_head)
+                with_head(normalise, attend_head)
+                for unit in units:
+                    copy_x(unit)
                 exponentials(step)
-            if in_range(step - ATTEND_LAG, H):
-                invert_sums(step - ATTEND_LAG)
-            if in_range(step - 2, H):
-                quantise_e(step - 2)
-            if in_range(step - PROJECT_LAG, H):
-                project(step - PROJECT_LAG)
-            if in_range(step - ATTEND_LAG, H):
-                attend(step - ATTEND_LAG)
-                normalise(step - ATTEND_LAG)
-            if in_range(step - PROJECT_LAG, H):
-                add_bias(step - PROJECT_LAG)
-            if in_range(step - X_START, 2):
-                quantise_x(2 * (step - X_START))
-                quantise_x(2 * (step - X_START) + 1)
-            if in_range(step - REGROUP_LAG, H):
-                regroup_w(step - REGROUP_LAG)
-            if in_range(step - REGROUP_LAG - 1, H):
-                quantise_w(step - REGROUP_LAG - 1)
-            if in_range(step - PROJECT_LAG, H):
-                quantise_v(step - PROJECT_LAG)
-            if in_range(step - 1, H):
-                turn_e(step - 1)
-            if in_range(step + 2, H):
-                turn_qk(step + 2)
-            if in_range(step + 1, H):
-                scores(step + 1)
+                with_head(regroup_w, weight_head, "vector")
+                with_head(quantise_v, project_head)
+                with_head(quantise_e, step - 2, 0)
+                with_head(quantise_e, step - 2, 1)
+                for unit in late_units + units:
+                    quantise_x(unit)
+                with_head(turn_e, step - 1, 0)
+                with_head(turn_e, step - 1, 1)
+                with_head(turn_qk, step + TURN_QK_AHEAD)
+                with_head(quantise_w, weight_head)
+                with_head(regroup_w, weight_head + 1, "gpsimd")
+                with_head(scores, step + 1)
+                for unit in x_last.get(step, ()):
+                    turn_x(unit)
+
+            a, b, c, d = range(H - 4, H)
+            regroup_w(d, "vector")
+            project(b, mx_ps, "v")
+            quantise_w(d)
+            copy_e(c, 0)
+            copy_e(c, 1)
+            attend(a, mx_ps, "ctx")
+            add_bias(b)
+            quantise_v(b)
+            quantise_e(c, 0)
+            quantise_e(c, 1)
+            turn_e(d, 0)
+            turn_e(d, 1)
+            for h in (a, b, c, d):
+                invert_sums(h)
+            normalise(a, 2)
+            project(c, score_ps, "score_high")
+            project(d, score_ps, "score_mid")
+            copy_e(d, 0)
+            copy_e(d, 1)
+            add_bias(c)
+            quantise_e(d, 0)
+            quantise_v(c)
+            quantise_e(d, 1)
+            add_bias(d)
+            attend(b, mx_ps, "ctx")
+            normalise(b)
+            quantise_v(d)
+            attend(c, mx_ps, "v")
+            attend(d, score_ps, "score_low")
+            normalise(c, 0)
+            normalise(d, 2)

@@ -41,7 +41,8 @@ TURN_QK_AHEAD = 2
 QUANTISE_W_LAG = 1
 PROJECT_LAG = 3
 ATTEND_LAG = PROJECT_LAG + 1
-GPSIMD_PASSES = 2
+ON_GPSIMD = slice(0, 3)
+ON_VECTOR = slice(3, PASSES)
 
 TILE_KEYS = sum((c + 1) * P for c in range(ROW_TILES))
 
@@ -107,19 +108,21 @@ def tile_selfattention_pa_kernel(tc, x, Wv, bv, q, k, out):
                 nc.sync.dma_start(out=w_raw[:, :, e, :], in_=w_rows[e, :, :, cols])
             w_raw_of[group] = w_raw
 
+        def load_x(u):
+            nc.sync.dma_start(
+                out=x_sb[:, 2 * u : 2 * u + 2, :].rearrange("m e k -> m (e k)"), in_=x_rows[:, u, :]
+            )
+
         x_sb = fixed.tile([P, ROW_TILES, D], BF16)
         bias_rows = consts.tile([P, D], BF16)
         with tc.manual_schedule(engines={mybir.EngineType.SP}):
             load_qk(0)
             load_qk(1)
-            for u in range(2):
-                nc.sync.dma_start(
-                    out=x_sb[:, 2 * u : 2 * u + 2, :].rearrange("m e k -> m (e k)"),
-                    in_=x_rows[:, u, :],
-                )
-                load_qk(2 + u)
+            load_x(0)
+            load_qk(2)
             load_chunk(0)
-            for h in range(4, 7):
+            load_x(1)
+            for h in range(3, 7):
                 load_qk(h)
             nc.sync.dma_start(out=bias_rows[:], in_=bv.partition_broadcast(P))
             for group in range(1, GROUPS):
@@ -235,8 +238,7 @@ def tile_selfattention_pa_kernel(tc, x, Wv, bv, q, k, out):
 
         def copy_x(unit):
             x_grouped = x_stage.tile([P, 2 * P * PACK], BF16, align_bytes=64, name="x_grouped")
-            copy = nc.scalar.copy if unit % 2 == 0 else nc.vector.tensor_copy
-            copy(
+            nc.scalar.copy(
                 out=x_grouped[:].bitcast(F32).rearrange("p (g m u) -> p g m u", g=2, u=2),
                 in_=x_bank_of[unit][:].rearrange("p (g u) m -> p g m u", u=2),
             )
@@ -251,18 +253,21 @@ def tile_selfattention_pa_kernel(tc, x, Wv, bv, q, k, out):
                 in_=x_grouped_of[unit][:],
             )
 
-        def regroup_w(h, engine):
+        def regroup_w(h, on_gpsimd, passes):
             group, member = divmod(h, GROUP)
             head_cols = slice(member * HD, (member + 1) * HD)
-            rows_of_pass = w_raw_of[group][:, :, :, head_cols].rearrange(
+            if h not in w_grouped_of:
+                w_grouped_of[h] = w_stage.tile(
+                    [P, PASSES, HD, PACK], BF16, align_bytes=64, name="w_grouped"
+                )
+            w_grouped = w_grouped_of[h][:, passes, :, :]
+            w_rows_of_pass = w_raw_of[group][:, :, :, head_cols].rearrange(
                 "p (g u) e n -> p g (u e) n", u=2
-            )
-            if engine == "gpsimd":
-                w_grouped = w_stage.tile([P, PASSES, HD, PACK], BF16, align_bytes=64, name="w_grouped")
-                w_grouped_of[h] = w_grouped
+            )[:, passes, :, :]
+            if on_gpsimd:
                 nc.gpsimd.tensor_scalar(
-                    out=w_grouped[:, :GPSIMD_PASSES, :, :],
-                    in0=rows_of_pass[:, :GPSIMD_PASSES, :, :].rearrange("p g t n -> p g n t"),
+                    out=w_grouped,
+                    in0=w_rows_of_pass.rearrange("p g t n -> p g n t"),
                     scalar1=1.0,
                     scalar2=0.0,
                     op0=ALU.mult,
@@ -270,10 +275,8 @@ def tile_selfattention_pa_kernel(tc, x, Wv, bv, q, k, out):
                 )
             else:
                 nc.vector.tensor_copy(
-                    out=w_grouped_of[h][:, GPSIMD_PASSES:, :, :].rearrange(
-                        "p g (c i) t -> p g c t i", i=4
-                    ),
-                    in_=rows_of_pass[:, GPSIMD_PASSES:, :, :].rearrange("p g t (c i) -> p g c t i", i=4),
+                    out=w_grouped.rearrange("p g (c i) t -> p g c t i", i=4),
+                    in_=w_rows_of_pass.rearrange("p g t (c i) -> p g c t i", i=4),
                 )
 
         def quantise_w(h):
@@ -373,8 +376,7 @@ def tile_selfattention_pa_kernel(tc, x, Wv, bv, q, k, out):
             e_grouped = stage.tile(
                 [P, 2 * P * PACK], BF16, align_bytes=64, name=("e_grouped_low", "e_grouped_high")[pair]
             )
-            copy = nc.vector.tensor_copy if h >= H - 2 and pair == 1 else nc.scalar.copy
-            copy(
+            nc.scalar.copy(
                 out=e_grouped[:].bitcast(F32).rearrange("p (c i u) -> p c i u", c=2, u=2),
                 in_=e_bank_of[h, pair][:].rearrange("p c u i -> p c i u"),
             )
@@ -474,8 +476,8 @@ def tile_selfattention_pa_kernel(tc, x, Wv, bv, q, k, out):
             if 0 <= h < H:
                 stage_of_head(h, *args)
 
-        x_first = {1: (2, 3), 2: (6, 7)}
-        x_last = {0: (0, 1), 1: (4, 5)}
+        x_first = {0: (0, 1), 1: (4, 5), 2: (6, 7)}
+        x_last = {0: (2, 3)}
 
         with tc.manual_schedule():
             turn_qk(0)
@@ -506,7 +508,7 @@ def tile_selfattention_pa_kernel(tc, x, Wv, bv, q, k, out):
                 for unit in units:
                     copy_x(unit)
                 exponentials(step)
-                with_head(regroup_w, weight_head, "vector")
+                with_head(regroup_w, weight_head, False, ON_VECTOR)
                 with_head(quantise_v, project_head)
                 with_head(quantise_e, step - 2, 0)
                 with_head(quantise_e, step - 2, 1)
@@ -516,39 +518,42 @@ def tile_selfattention_pa_kernel(tc, x, Wv, bv, q, k, out):
                 with_head(turn_e, step - 1, 1)
                 with_head(turn_qk, step + TURN_QK_AHEAD)
                 with_head(quantise_w, weight_head)
-                with_head(regroup_w, weight_head + 1, "gpsimd")
+                if step < H - 1:
+                    regroup_w(step, True, ON_GPSIMD)
                 with_head(scores, step + 1)
                 for unit in x_last.get(step, ()):
                     turn_x(unit)
 
             a, b, c, d = range(H - 4, H)
-            regroup_w(d, "vector")
             project(b, mx_ps, "v")
+            regroup_w(d, False, slice(0, PASSES))
             quantise_w(d)
             copy_e(c, 0)
             copy_e(c, 1)
             attend(a, mx_ps, "ctx")
+            invert_sums(a)
             add_bias(b)
-            quantise_v(b)
             quantise_e(c, 0)
+            quantise_v(b)
             quantise_e(c, 1)
+            normalise(a)
             turn_e(d, 0)
             turn_e(d, 1)
-            for h in (a, b, c, d):
-                invert_sums(h)
-            normalise(a, 2)
             project(c, score_ps, "score_high")
             project(d, score_ps, "score_mid")
             copy_e(d, 0)
             copy_e(d, 1)
+            invert_sums(b)
             add_bias(c)
             quantise_e(d, 0)
             quantise_v(c)
             quantise_e(d, 1)
+            invert_sums(c)
+            invert_sums(d)
             add_bias(d)
+            quantise_v(d)
             attend(b, mx_ps, "ctx")
             normalise(b)
-            quantise_v(d)
             attend(c, mx_ps, "v")
             attend(d, score_ps, "score_low")
             normalise(c, 0)

@@ -238,7 +238,8 @@ def tile_selfattention_pa_kernel(tc, x, Wv, bv, q, k, out):
 
         def copy_x(unit):
             x_grouped = x_stage.tile([P, 2 * P * PACK], BF16, align_bytes=64, name="x_grouped")
-            nc.scalar.copy(
+            copy = nc.scalar.copy if unit % 2 == 0 else nc.vector.tensor_copy
+            copy(
                 out=x_grouped[:].bitcast(F32).rearrange("p (g m u) -> p g m u", g=2, u=2),
                 in_=x_bank_of[unit][:].rearrange("p (g u) m -> p g m u", u=2),
             )
@@ -302,34 +303,34 @@ def tile_selfattention_pa_kernel(tc, x, Wv, bv, q, k, out):
             nc.scalar.copy(out=qk_t[:], in_=qk_bank_of[h][:])
             qk_turned[h] = qk_t
 
-        def scores(h):
+        def scores(h, tiles):
             qk_t = qk_turned[h]
-            score_low = score_ps.tile([P, S], F32, name="score_low")
-            score_mid = score_ps.tile([P, S], F32, name="score_mid")
-            score_high = score_ps.tile([P, S], F32, name="score_high")
-            score_of = [
-                score_low[:, :P],
-                score_low[:, P : 3 * P],
-                score_mid[:, : 3 * P],
-                score_high[:, :],
-            ]
-            for c in range(ROW_TILES):
+            if h not in score_of_head:
+                score_low = score_ps.tile([P, S], F32, name="score_low")
+                score_mid = score_ps.tile([P, S], F32, name="score_mid")
+                score_high = score_ps.tile([P, S], F32, name="score_high")
+                score_of_head[h] = [
+                    score_low[:, :P],
+                    score_low[:, P : 3 * P],
+                    score_mid[:, : 3 * P],
+                    score_high[:, :],
+                ]
+            for c in tiles:
                 keys = (c + 1) * P
                 nc.tensor.matmul(
-                    score_of[c],
+                    score_of_head[h][c],
                     lhsT=qk_t[:, c, :],
                     rhs=qk_t[:, ROW_TILES : ROW_TILES + c + 1, :].rearrange("d c j -> d (c j)"),
                     start=True,
                     stop=False,
                 )
                 nc.tensor.matmul(
-                    score_of[c],
+                    score_of_head[h][c],
                     lhsT=bias_lhsT[:, h, :],
                     rhs=bias_rhs[:, S - keys :],
                     start=False,
                     stop=True,
                 )
-            score_of_head[h] = score_of
 
         def row_maxima(h):
             scaled = scaled_pool.tile([P, TILE_KEYS], F32, name="scaled")
@@ -448,21 +449,27 @@ def tile_selfattention_pa_kernel(tc, x, Wv, bv, q, k, out):
             ctx_acc_of[h] = ctx_acc
 
         def invert_sums(h):
-            columns = slice(h * ROW_TILES, (h + 1) * ROW_TILES)
+            columns = slice(h * ROW_TILES, (h + 2) * ROW_TILES)
             nc.vector.reciprocal(out=inv_sum[:, columns], in_=row_sum[:, columns])
 
-        def normalise(h, on_scalar=ROW_TILES):
+        def normalise_last(h):
             ctx_sb = out_pool.tile([P, ROW_TILES, HD], F32, name="ctx_sb")
-            if on_scalar < ROW_TILES:
-                rest = slice(on_scalar, ROW_TILES)
-                inverse = inv_sum[:, h * ROW_TILES + on_scalar : (h + 1) * ROW_TILES]
+            for half in range(2):
+                tiles = slice(2 * half, 2 * half + 2)
+                columns = slice(h * ROW_TILES + 2 * half, h * ROW_TILES + 2 * half + 2)
                 nc.vector.tensor_tensor(
-                    out=ctx_sb[:, rest, :],
-                    in0=ctx_acc_of[h][:, rest, :],
-                    in1=inverse.unsqueeze(2).to_broadcast([P, ROW_TILES - on_scalar, HD]),
+                    out=ctx_sb[:, tiles, :],
+                    in0=ctx_acc_of[h][:, tiles, :],
+                    in1=inv_sum[:, columns].unsqueeze(2).to_broadcast([P, 2, HD]),
                     op=ALU.mult,
                 )
-            for c in range(on_scalar):
+                nc.sync.dma_start(
+                    out=out_rows[:, tiles, h * HD : (h + 1) * HD], in_=ctx_sb[:, tiles, :]
+                )
+
+        def normalise(h):
+            ctx_sb = out_pool.tile([P, ROW_TILES, HD], F32, name="ctx_sb")
+            for c in range(ROW_TILES):
                 column = h * ROW_TILES + c
                 nc.scalar.activation(
                     out=ctx_sb[:, c, :],
@@ -485,7 +492,7 @@ def tile_selfattention_pa_kernel(tc, x, Wv, bv, q, k, out):
             turn_qk(1)
             for cc in range(2):
                 nc.tensor.transpose(e_low[:, cc, 1, :], zeros[:], ident_f32[:])
-            scores(0)
+            scores(0, range(ROW_TILES))
             for step in range(H):
                 weight_head = step - QUANTISE_W_LAG
                 project_head = step - PROJECT_LAG
@@ -494,7 +501,8 @@ def tile_selfattention_pa_kernel(tc, x, Wv, bv, q, k, out):
                 units = x_first.get(step, ())
                 for unit in late_units:
                     copy_x(unit)
-                with_head(invert_sums, attend_head)
+                if attend_head % 2 == 0:
+                    with_head(invert_sums, attend_head)
                 with_head(project, project_head, mx_ps, "v")
                 with_head(attend, attend_head, mx_ps, "ctx")
                 for unit in units:
@@ -504,23 +512,24 @@ def tile_selfattention_pa_kernel(tc, x, Wv, bv, q, k, out):
                 with_head(copy_e, step - 2, 1)
                 row_maxima(step)
                 with_head(add_bias, project_head)
-                with_head(normalise, attend_head)
                 for unit in units:
                     copy_x(unit)
                 exponentials(step)
+                with_head(normalise, attend_head)
                 with_head(regroup_w, weight_head, False, ON_VECTOR)
                 with_head(quantise_v, project_head)
                 with_head(quantise_e, step - 2, 0)
                 with_head(quantise_e, step - 2, 1)
                 for unit in late_units + units:
                     quantise_x(unit)
+                with_head(turn_qk, step + TURN_QK_AHEAD)
+                with_head(scores, step + 1, (0, 1))
                 with_head(turn_e, step - 1, 0)
                 with_head(turn_e, step - 1, 1)
-                with_head(turn_qk, step + TURN_QK_AHEAD)
                 with_head(quantise_w, weight_head)
                 if step < H - 1:
                     regroup_w(step, True, ON_GPSIMD)
-                with_head(scores, step + 1)
+                with_head(scores, step + 1, (2, 3))
                 for unit in x_last.get(step, ()):
                     turn_x(unit)
 
@@ -530,31 +539,29 @@ def tile_selfattention_pa_kernel(tc, x, Wv, bv, q, k, out):
             quantise_w(d)
             copy_e(c, 0)
             copy_e(c, 1)
+            project(c, score_ps, "score_high")
             attend(a, mx_ps, "ctx")
-            invert_sums(a)
             add_bias(b)
             quantise_e(c, 0)
+            invert_sums(a)
             quantise_v(b)
             quantise_e(c, 1)
             normalise(a)
             turn_e(d, 0)
             turn_e(d, 1)
-            project(c, score_ps, "score_high")
             project(d, score_ps, "score_mid")
             copy_e(d, 0)
             copy_e(d, 1)
-            invert_sums(b)
             add_bias(c)
-            quantise_e(d, 0)
-            quantise_v(c)
-            quantise_e(d, 1)
             invert_sums(c)
-            invert_sums(d)
+            quantise_v(c)
             add_bias(d)
+            quantise_e(d, 0)
             quantise_v(d)
+            quantise_e(d, 1)
             attend(b, mx_ps, "ctx")
             normalise(b)
             attend(c, mx_ps, "v")
+            normalise(c)
             attend(d, score_ps, "score_low")
-            normalise(c, 0)
-            normalise(d, 2)
+            normalise_last(d)

from contextlib import ExitStack

import concourse.mybir as mybir
from concourse.masks import make_identity

F32 = mybir.dt.float32
BF16 = mybir.dt.bfloat16
I32 = mybir.dt.int32
U32 = mybir.dt.uint32
U8 = mybir.dt.uint8
FP8X4 = mybir.dt.float8_e4m3fn_x4
ALU = mybir.AluOpType
ACT = mybir.ActivationFunctionType

P = 128
S = 512
D = 2048
H = 16
HD = 128
PACK = 4
K_PASS = P * PACK
PASSES = D // K_PASS
ROW_TILES = S // P
GROUP = 4
GROUPS = H // GROUP
CHUNK = GROUP * HD
PLANES = D // (2 * P)

SCALE = 1.0 / HD**0.5
KEY_CENTRE = S // 2
QUADRANT = 32
MASK_ROWS = P // 2
FAINT = 2.0**-78
MASK_EVEN = -(2.0**48)
MASK_ODD = -(2.0**126)

FLOPS = 2 * S * D * D + 2 * 2 * H * S * S * HD


TURN_QK_AHEAD = 2
QUANTISE_W_LAG = 1
PROJECT_LAG = 3
ATTEND_LAG = PROJECT_LAG + 1
ON_GPSIMD = slice(0, 3)
ON_VECTOR = slice(3, PASSES)

TILE_KEYS = sum((c + 1) * P for c in range(ROW_TILES))


def key_columns(c):
    start = sum((b + 1) * P for b in range(c))
    return slice(start, start + (c + 1) * P)


def tile_selfattention_pa_kernel(tc, x, Wv, bv, q, k, out):
    nc = tc.nc

    with ExitStack() as ctx:
        consts = ctx.enter_context(tc.tile_pool(name="consts", bufs=1))
        fixed = ctx.enter_context(tc.tile_pool(name="fixed", bufs=1))
        w_raw_pool = ctx.enter_context(tc.tile_pool(name="w_raw", bufs=GROUPS))
        qk_raw_pool = ctx.enter_context(tc.tile_pool(name="qk_raw", bufs=H))
        stage = ctx.enter_context(tc.tile_pool(name="stage", bufs=2))
        x_stage = ctx.enter_context(tc.tile_pool(name="x_stage", bufs=4))
        w_stage = ctx.enter_context(tc.tile_pool(name="w_stage", bufs=1))
        scaled_pool = ctx.enter_context(tc.tile_pool(name="scaled", bufs=2))
        e_mx_pool = ctx.enter_context(tc.tile_pool(name="e_mx", bufs=ATTEND_LAG))
        w_mx_pool = ctx.enter_context(tc.tile_pool(name="w_mx", bufs=3))
        out_pool = ctx.enter_context(tc.tile_pool(name="out", bufs=4))
        head_pool = ctx.enter_context(tc.tile_pool(name="head", bufs=2))
        score_ps = ctx.enter_context(tc.psum_pool(name="score_ps", bufs=1))
        turn_ps = ctx.enter_context(tc.psum_pool(name="turn_ps", bufs=1))
        mx_ps = ctx.enter_context(tc.psum_pool(name="mx_ps", bufs=1))

        q_rows = q.rearrange("b h (c p) d -> p (b h) c d", p=P)
        k_rows = k.rearrange("b h (c p) d -> p (b h) c d", p=P)
        w_rows = Wv.rearrange("(l p e) n -> e p l n", l=PLANES, e=2)
        x_rows = x.rearrange("b (u m e) k -> m (b u) (e k)", u=2, e=2)
        out_rows = out.rearrange("b (c a) n -> a (b c) n", a=P)

        qk_sb = {}
        qk_turned = {}
        w_raw_of = {}
        w_grouped_of = {}
        w_mx_of = {}
        e_mx_of = {}
        qk_bank_of = {}
        score_of_head = {}
        scaled_of = {}
        e_bank_of = {}
        e_grouped_of = {}
        v_acc_of = {}
        v_grouped_of = {}
        ctx_acc_of = {}
        v_mx_of = {}

        def load_qk(h):
            q_sb = qk_raw_pool.tile([P, ROW_TILES, HD], BF16, name="q_sb")
            k_sb = qk_raw_pool.tile([P, ROW_TILES, HD], BF16, name="k_sb")
            nc.sync.dma_start(out=q_sb[:], in_=q_rows[:, h, :, :])
            nc.sync.dma_start(out=k_sb[:], in_=k_rows[:, h, :, :])
            qk_sb[h] = (q_sb, k_sb)

        def load_chunk(group):
            cols = slice(group * CHUNK, (group + 1) * CHUNK)
            w_raw = w_raw_pool.tile([P, PLANES, 2, CHUNK], BF16, name="w_raw")
            for e in range(2):
                nc.sync.dma_start(out=w_raw[:, :, e, :], in_=w_rows[e, :, :, cols])
            w_raw_of[group] = w_raw

        def load_x(u):
            nc.sync.dma_start(
                out=x_sb[:, 2 * u : 2 * u + 2, :].rearrange("m e k -> m (e k)"), in_=x_rows[:, u, :]
            )

        x_sb = fixed.tile([P, ROW_TILES, D], BF16)
        bias_rows = consts.tile([P, D], BF16)
        with tc.manual_schedule(engines={mybir.EngineType.SP}):
            load_qk(0)
            load_qk(1)
            load_x(0)
            load_qk(2)
            load_chunk(0)
            load_x(1)
            for h in range(3, 7):
                load_qk(h)
            nc.sync.dma_start(out=bias_rows[:], in_=bv.partition_broadcast(P))
            for group in range(1, GROUPS):
                load_chunk(group)
                for h in range(GROUP * group + 3, min(GROUP * group + 7, H)):
                    load_qk(h)

        ident_bf = consts.tile([P, P], BF16)
        query_mask = consts.tile([P, P], F32)
        bias_rhs = consts.tile([P, S], BF16)
        ident_f32 = consts.tile([P, P], F32)
        nc.vector.memset(ident_bf[:], 0.0)
        nc.vector.memset(query_mask[:], 1.0)
        nc.vector.memset(bias_rhs[:MASK_ROWS, :], 0.0)
        nc.vector.memset(ident_f32[:], 0.0)
        make_identity(nc, ident_bf[:], nomemset=True)

        nc.gpsimd.affine_select(
            out=query_mask[:],
            in_=query_mask[:],
            compare_op=ALU.is_gt,
            fill=0.0,
            base=0,
            pattern=[[-1, P]],
            channel_multiplier=2,
        )
        nc.gpsimd.affine_select(
            out=query_mask[:],
            in_=query_mask[:],
            compare_op=ALU.not_equal,
            fill=FAINT,
            base=0,
            pattern=[[-1, P]],
            channel_multiplier=2,
        )
        key_numbers = consts.tile([P, S], I32)
        nc.gpsimd.iota(key_numbers[:], pattern=[[1, S]], base=-KEY_CENTRE, channel_multiplier=0)
        for odd, fill in ((0, MASK_EVEN), (1, MASK_ODD)):
            nc.gpsimd.affine_select(
                out=bias_rhs[:MASK_ROWS, :],
                in_=bias_rhs[:MASK_ROWS, :],
                compare_op=ALU.not_equal,
                fill=fill,
                base=-(S - P) - odd,
                pattern=[[1, S]],
                channel_multiplier=-2,
            )
        make_identity(nc, ident_f32[:], nomemset=True)

        slope = consts.tile([P, H // 2, 2], F32)
        for n in range(H // 2):
            nc.vector.memset(slope[:, n, :], 2.0 ** (3 - n))
        nc.vector.tensor_scalar(
            out=slope[:, :, 1], in0=slope[:, :, 1], scalar1=2.0**-0.5, scalar2=None, op0=ALU.mult
        )
        slope = slope[:].rearrange("p n i -> p (n i)")
        slope_high = consts.tile([P, H], BF16)
        nc.vector.tensor_copy(out=slope_high[:], in_=slope)
        slope_rest = consts.tile([P, H], F32)
        nc.vector.tensor_tensor(out=slope_rest[:], in0=slope, in1=slope_high[:], op=ALU.subtract)

        bias_lhsT = consts.tile([P, H, P], BF16)
        high_rows = slice(MASK_ROWS, MASK_ROWS + QUADRANT)
        rest_rows = slice(MASK_ROWS + QUADRANT, P)
        nc.vector.tensor_copy(
            out=bias_lhsT[high_rows, :, :],
            in_=slope_high[high_rows, :].unsqueeze(2).to_broadcast([QUADRANT, H, P]),
        )
        nc.vector.tensor_copy(
            out=bias_lhsT[rest_rows, :, :],
            in_=slope_rest[rest_rows, :].unsqueeze(2).to_broadcast([QUADRANT, H, P]),
        )
        nc.scalar.copy(
            out=bias_lhsT[:MASK_ROWS, :, :],
            in_=query_mask[:MASK_ROWS, :].unsqueeze(1).to_broadcast([MASK_ROWS, H, P]),
        )
        nc.vector.tensor_scalar(
            out=bias_rhs[MASK_ROWS:, :],
            in0=key_numbers[MASK_ROWS:, :],
            scalar1=1.0 / QUADRANT,
            scalar2=None,
            op0=ALU.mult,
        )

        e_rows = [fixed.tile([P, ROW_TILES, S], BF16, name="e_rows%d" % par) for par in range(2)]
        for par in range(2):
            for c in (0, 2):
                nc.gpsimd.memset(e_rows[par][:, c, (c + 1) * P : (c + 2) * P], 0.0)
        zeros = consts.tile([P, P], F32)
        nc.gpsimd.memset(zeros[:], 0.0)
        e_low = turn_ps.tile([P, 2, 2, P], F32, name="e_low")
        exp_probe = consts.tile([P, 1], F32)
        nc.scalar.activation(out=exp_probe[:], in_=ident_f32[:, :1], func=ACT.Exp)

        neg_max = fixed.tile([P, H * ROW_TILES], F32)
        row_sum = fixed.tile([P, H * ROW_TILES], F32)
        inv_sum = fixed.tile([P, H * ROW_TILES], F32)
        x_bank_of = {}
        x_grouped_of = {}
        x_codes = fixed.tile([P, ROW_TILES, PASSES, P], U32, align_bytes=64)
        x_scales = fixed.tile([P, ROW_TILES, PASSES, P], U8, align_bytes=64)

        def turn_x(unit):
            t, half = divmod(unit, 2)
            x_words = x_sb[:, t, :].bitcast(F32)
            turned = mx_ps.tile([P, 4, P], F32, name="x_turned", tag=("v", "ctx")[half])
            for w in range(4):
                plane = 4 * half + w
                nc.tensor.transpose(
                    turned[:, w, :], x_words[:, plane * P : (plane + 1) * P], ident_f32[:]
                )
            x_bank_of[unit] = turned

        def copy_x(unit):
            x_grouped = x_stage.tile([P, 2 * P * PACK], BF16, align_bytes=64, name="x_grouped")
            copy = nc.scalar.copy if unit % 2 == 0 else nc.vector.tensor_copy
            copy(
                out=x_grouped[:].bitcast(F32).rearrange("p (g m u) -> p g m u", g=2, u=2),
                in_=x_bank_of[unit][:].rearrange("p (g u) m -> p g m u", u=2),
            )
            x_grouped_of[unit] = x_grouped

        def quantise_x(unit):
            t, half = divmod(unit, 2)
            passes = slice(2 * half, 2 * half + 2)
            nc.vector.quantize_mx(
                out=x_codes[:, t, passes, :].rearrange("p g m -> p (g m)").bitcast(FP8X4),
                scales=x_scales[:, t, passes, :].rearrange("p g m -> p (g m)"),
                in_=x_grouped_of[unit][:],
            )

        def regroup_w(h, on_gpsimd, passes):
            group, member = divmod(h, GROUP)
            head_cols = slice(member * HD, (member + 1) * HD)
            if h not in w_grouped_of:
                w_grouped_of[h] = w_stage.tile(
                    [P, PASSES, HD, PACK], BF16, align_bytes=64, name="w_grouped"
                )
            w_grouped = w_grouped_of[h][:, passes, :, :]
            w_rows_of_pass = w_raw_of[group][:, :, :, head_cols].rearrange(
                "p (g u) e n -> p g (u e) n", u=2
            )[:, passes, :, :]
            if on_gpsimd:
                nc.gpsimd.tensor_scalar(
                    out=w_grouped,
                    in0=w_rows_of_pass.rearrange("p g t n -> p g n t"),
                    scalar1=1.0,
                    scalar2=0.0,
                    op0=ALU.mult,
                    op1=ALU.add,
                )
            else:
                nc.vector.tensor_copy(
                    out=w_grouped.rearrange("p g (c i) t -> p g c t i", i=4),
                    in_=w_rows_of_pass.rearrange("p g t (c i) -> p g c t i", i=4),
                )

        def quantise_w(h):
            w_codes = w_mx_pool.tile([P, PASSES, HD], U32, align_bytes=64, name="w_codes")
            w_scales = w_mx_pool.tile([P, PASSES, HD], U8, align_bytes=64, name="w_scales")
            nc.vector.quantize_mx(
                out=w_codes[:].rearrange("p g n -> p (g n)").bitcast(FP8X4),
                scales=w_scales[:].rearrange("p g n -> p (g n)"),
                in_=w_grouped_of[h][:].rearrange("p g n t -> p (g n t)"),
            )
            w_mx_of[h] = (w_codes, w_scales)

        def turn_qk(h):
            q_sb, k_sb = qk_sb[h]
            turned = turn_ps.tile([P, 2 * ROW_TILES, P], BF16, name="qk_bank")
            for c in range(ROW_TILES):
                nc.tensor.transpose(turned[:, c, :], q_sb[:, c, :], ident_bf[:])
                nc.tensor.transpose(turned[:, ROW_TILES + c, :], k_sb[:, c, :], ident_bf[:])
            qk_bank_of[h] = turned

        def copy_qk(h):
            qk_t = head_pool.tile([P, 2 * ROW_TILES, P], BF16, name="qk_t")
            nc.scalar.copy(out=qk_t[:], in_=qk_bank_of[h][:])
            qk_turned[h] = qk_t

        def scores(h, tiles):
            qk_t = qk_turned[h]
            if h not in score_of_head:
                score_low = score_ps.tile([P, S], F32, name="score_low")
                score_mid = score_ps.tile([P, S], F32, name="score_mid")
                score_high = score_ps.tile([P, S], F32, name="score_high")
                score_of_head[h] = [
                    score_low[:, :P],
                    score_low[:, P : 3 * P],
                    score_mid[:, : 3 * P],
                    score_high[:, :],
                ]
            for c in tiles:
                keys = (c + 1) * P
                nc.tensor.matmul(
                    score_of_head[h][c],
                    lhsT=qk_t[:, c, :],
                    rhs=qk_t[:, ROW_TILES : ROW_TILES + c + 1, :].rearrange("d c j -> d (c j)"),
                    start=True,
                    stop=False,
                )
                nc.tensor.matmul(
                    score_of_head[h][c],
                    lhsT=bias_lhsT[:, h, :],
                    rhs=bias_rhs[:, S - keys :],
                    start=False,
                    stop=True,
                )

        def row_maxima(h):
            scaled = scaled_pool.tile([P, TILE_KEYS], F32, name="scaled")
            for c in range(ROW_TILES):
                column = h * ROW_TILES + c
                nc.vector.tensor_scalar(
                    out=scaled[:, key_columns(c)],
                    in0=score_of_head[h][c],
                    scalar1=-SCALE,
                    scalar2=None,
                    op0=ALU.mult,
                    op1=ALU.min,
                    accum_out=neg_max[:, column : column + 1],
                )
            scaled_of[h] = scaled

        def exponentials(h):
            for c in range(ROW_TILES):
                keys = (c + 1) * P
                column = h * ROW_TILES + c
                nc.scalar.activation(
                    out=e_rows[h % 2][:, c, :keys],
                    in_=scaled_of[h][:, key_columns(c)],
                    func=ACT.Exp,
                    bias=neg_max[:, column : column + 1],
                    scale=-1.0,
                    accum_out=row_sum[:, column : column + 1],
                )

        def turn_e(h, pair):
            if pair == 0:
                turned = e_low
            else:
                turned = turn_ps.tile([P, 2, 2, P], F32, name="e_high")
            for cc in range(2):
                e_words = e_rows[h % 2][:, 2 * pair + cc, :].bitcast(F32)
                for u in range(pair + 1):
                    nc.tensor.transpose(
                        turned[:, cc, u, :], e_words[:, u * P : (u + 1) * P], ident_f32[:]
                    )
            e_bank_of[h, pair] = turned

        def copy_e(h, pair):
            e_grouped = stage.tile(
                [P, 2 * P * PACK], BF16, align_bytes=64, name=("e_grouped_low", "e_grouped_high")[pair]
            )
            nc.scalar.copy(
                out=e_grouped[:].bitcast(F32).rearrange("p (c i u) -> p c i u", c=2, u=2),
                in_=e_bank_of[h, pair][:].rearrange("p c u i -> p c i u"),
            )
            e_grouped_of[h, pair] = e_grouped

        def quantise_e(h, pair):
            if pair == 0:
                e_codes = e_mx_pool.tile([P, ROW_TILES, P], U32, align_bytes=64, name="e_codes")
                e_scales = e_mx_pool.tile([P, ROW_TILES, P], U8, align_bytes=64, name="e_scales")
                e_mx_of[h] = (e_codes, e_scales)
            e_codes, e_scales = e_mx_of[h]
            tiles = slice(2 * pair, 2 * pair + 2)
            nc.vector.quantize_mx(
                out=e_codes[:, tiles, :].rearrange("p c i -> p (c i)").bitcast(FP8X4),
                scales=e_scales[:, tiles, :].rearrange("p c i -> p (c i)"),
                in_=e_grouped_of[h, pair][:],
            )

        def project(h, pool, bank):
            w_codes, w_scales = w_mx_of[h]
            v_acc = pool.tile([P, ROW_TILES, HD], F32, name="v_acc", tag=bank)
            for t in range(ROW_TILES):
                for g in range(PASSES):
                    nc.tensor.matmul_mx(
                        out=v_acc[:, t, :],
                        lhsT=x_codes[:, t, g, :].bitcast(FP8X4),
                        lhsT_scale=x_scales[:, t, g, :],
                        rhs=w_codes[:, g, :].bitcast(FP8X4),
                        rhs_scale=w_scales[:, g, :],
                        start=(g == 0),
                        stop=(g == PASSES - 1),
                    )
            v_acc_of[h] = v_acc

        def add_bias(h):
            v_grouped = stage.tile([P, HD, PACK], BF16, align_bytes=64, name="v_grouped")
            nc.vector.tensor_tensor(
                out=v_grouped[:],
                in0=v_acc_of[h][:].rearrange("m t d -> m d t"),
                in1=bias_rows[:, h * HD : (h + 1) * HD].unsqueeze(2).to_broadcast([P, HD, PACK]),
                op=ALU.add,
            )
            v_grouped_of[h] = v_grouped

        def quantise_v(h):
            v_codes = head_pool.tile([P, HD], U32, align_bytes=64, name="v_codes")
            v_scales = head_pool.tile([P, HD], U8, align_bytes=64, name="v_scales")
            nc.vector.quantize_mx(
                out=v_codes[:].bitcast(FP8X4),
                scales=v_scales[:],
                in_=v_grouped_of[h][:].rearrange("m d t -> m (d t)"),
            )
            v_mx_of[h] = (v_codes, v_scales)

        def attend(h, pool, bank):
            e_codes, e_scales = e_mx_of[h]
            v_codes, v_scales = v_mx_of[h]
            ctx_acc = pool.tile([P, ROW_TILES, HD], F32, name="ctx_acc", tag=bank)
            for c in range(ROW_TILES):
                nc.tensor.matmul_mx(
                    out=ctx_acc[:, c, :],
                    lhsT=e_codes[:, c, :].bitcast(FP8X4),
                    lhsT_scale=e_scales[:, c, :],
                    rhs=v_codes[:].bitcast(FP8X4),
                    rhs_scale=v_scales[:],
                    start=True,
                    stop=True,
                )
            ctx_acc_of[h] = ctx_acc

        def invert_sums(h):
            columns = slice(h * ROW_TILES, (h + 2) * ROW_TILES)
            nc.vector.reciprocal(out=inv_sum[:, columns], in_=row_sum[:, columns])

        def normalise_last(h):
            ctx_sb = out_pool.tile([P, ROW_TILES, HD], F32, name="ctx_sb")
            for half in range(2):
                tiles = slice(2 * half, 2 * half + 2)
                columns = slice(h * ROW_TILES + 2 * half, h * ROW_TILES + 2 * half + 2)
                nc.vector.tensor_tensor(
                    out=ctx_sb[:, tiles, :],
                    in0=ctx_acc_of[h][:, tiles, :],
                    in1=inv_sum[:, columns].unsqueeze(2).to_broadcast([P, 2, HD]),
                    op=ALU.mult,
                )
                nc.sync.dma_start(
                    out=out_rows[:, tiles, h * HD : (h + 1) * HD], in_=ctx_sb[:, tiles, :]
                )

        def normalise(h):
            ctx_sb = out_pool.tile([P, ROW_TILES, HD], F32, name="ctx_sb")
            for c in range(ROW_TILES):
                column = h * ROW_TILES + c
                nc.scalar.activation(
                    out=ctx_sb[:, c, :],
                    in_=ctx_acc_of[h][:, c, :],
                    func=ACT.Copy,
                    scale=inv_sum[:, column : column + 1],
                )
            nc.sync.dma_start(out=out_rows[:, :, h * HD : (h + 1) * HD], in_=ctx_sb[:])

        def with_head(stage_of_head, h, *args):
            if 0 <= h < H:
                stage_of_head(h, *args)

        x_first = {0: (0, 1), 1: (4, 5), 2: (6, 7)}
        x_last = {0: (2, 3)}

        with tc.manual_schedule():
            turn_qk(0)
            copy_qk(0)
            turn_qk(1)
            for cc in range(2):
                nc.tensor.transpose(e_low[:, cc, 1, :], zeros[:], ident_f32[:])
            scores(0, range(ROW_TILES))
            for step in range(H):
                weight_head = step - QUANTISE_W_LAG
                project_head = step - PROJECT_LAG
                attend_head = step - ATTEND_LAG
                late_units = x_last.get(step - 1, ())
                units = x_first.get(step, ())
                for unit in late_units:
                    copy_x(unit)
                if attend_head % 2 == 0:
                    with_head(invert_sums, attend_head)
                with_head(project, project_head, mx_ps, "v")
                with_head(attend, attend_head, mx_ps, "ctx")
                for unit in units:
                    turn_x(unit)
                with_head(copy_qk, step + 1)
                with_head(copy_e, step - 2, 0)
                with_head(copy_e, step - 2, 1)
                row_maxima(step)
                with_head(add_bias, project_head)
                for unit in units:
                    copy_x(unit)
                exponentials(step)
                with_head(normalise, attend_head)
                with_head(regroup_w, weight_head, False, ON_VECTOR)
                with_head(quantise_v, project_head)
                with_head(quantise_e, step - 2, 0)
                with_head(quantise_e, step - 2, 1)
                for unit in late_units + units:
                    quantise_x(unit)
                with_head(turn_qk, step + TURN_QK_AHEAD)
                with_head(scores, step + 1, (0, 1))
                with_head(turn_e, step - 1, 0)
                with_head(turn_e, step - 1, 1)
                with_head(quantise_w, weight_head)
                if step < H - 1:
                    regroup_w(step, True, ON_GPSIMD)
                with_head(scores, step + 1, (2, 3))
                for unit in x_last.get(step, ()):
                    turn_x(unit)

            a, b, c, d = range(H - 4, H)
            project(b, mx_ps, "v")
            regroup_w(d, False, slice(0, PASSES))
            quantise_w(d)
            copy_e(c, 0)
            copy_e(c, 1)
            project(c, score_ps, "score_high")
            attend(a, mx_ps, "ctx")
            add_bias(b)
            quantise_e(c, 0)
            invert_sums(a)
            quantise_v(b)
            quantise_e(c, 1)
            normalise(a)
            turn_e(d, 0)
            turn_e(d, 1)
            project(d, score_ps, "score_mid")
            copy_e(d, 0)
            copy_e(d, 1)
            add_bias(c)
            invert_sums(c)
            quantise_v(c)
            add_bias(d)
            quantise_e(d, 0)
            quantise_v(d)
            quantise_e(d, 1)
            attend(b, mx_ps, "ctx")
            normalise(b)
            attend(c, mx_ps, "v")
            normalise(c)
            attend(d, score_ps, "score_low")
            normalise_last(d)
